import numpy as np
import ml_dtypes


def mxq(x, axis, fmt="e4m3"):
    dtype, down = {"e4m3": (ml_dtypes.float8_e4m3fn, 7), "e5m2": (ml_dtypes.float8_e5m2, 14)}[fmt]
    v = np.moveaxis(np.asarray(x, np.float32).astype(ml_dtypes.bfloat16).astype(np.float64), axis, -1)
    blocks = v.reshape(v.shape[:-1] + (-1, 32))
    amax = np.abs(blocks).max(-1, keepdims=True)
    byte = np.maximum(np.where(amax > 0, np.frexp(amax)[1] - 1 + 127, 0) - down, 1)
    scale = np.exp2(byte - 127.0)
    codes = (blocks / scale).astype(np.float32).astype(dtype).astype(np.float64)
    return np.moveaxis((codes * scale).reshape(v.shape), -1, axis)


WIDE = False


def mx_kscale(k):
    if not WIDE:
        return np.ones(k)
    levels = np.array([10, -10, 5, -5, 0])
    a = np.random.permutation(np.resize(levels, k // 512 * 4)).reshape(k // 512, 4)
    idx = np.arange(k)
    return np.exp2(a[idx // 512, idx % 128 // 32])


BF16 = ml_dtypes.bfloat16


def bf(x):
    return np.asarray(x, np.float32).astype(BF16)


def f64(x):
    return np.asarray(x).astype(np.float64)


N, F, H, O, D = 2048, 512, 4, 128, 128


def setup_inputs():
    s = mx_kscale(F)
    keep = np.random.random((N, 1)) >= 0.1
    linked = np.random.random((N, 1)) >= 0.1
    edge = np.random.randint(0, 2, (1, N, N)) * linked
    return {"h": bf(np.random.standard_normal((1, N, F)) * keep * s),
            "a": bf(edge * (0.5 + np.random.random((1, N, N)))),
            "kernel": bf(np.random.standard_normal((H, F, O)) * 2.0 / np.sqrt(F) / s[:, None]),
            "f_self": bf(np.random.standard_normal((H, N, D)) * 1.2),
            "f_other": bf(np.random.standard_normal((H, N, D)) * 1.2)}


def reference(h, a, kernel, f_self, f_other):
    x = f64(h)[0]
    adj = f64(a)[0]
    feats = mxq(x, 1, "e4m3") @ mxq(f64(kernel), 1, "e4m3")
    dense = f64(f_self) @ f64(f_other).transpose(0, 2, 1)
    masked = adj[None] * dense
    masked = np.where(masked >= 0, masked, 0.2 * masked)
    masked = masked / np.sqrt(D)
    z = masked + np.where(adj == 0, -1e9, 0.0)[None]
    e = np.exp(z - z.max(-1, keepdims=True))
    den = e.sum(-1, keepdims=True)
    em = e * (adj != 0)[None]
    nf = (mxq(em, 2, "e4m3") @ mxq(feats, 1, "e4m3")) / den
    nf = np.maximum(nf, 0.0)
    row_mask = (np.sum((x != 0) * 1.0, axis=-1, keepdims=True) > 0) * 1.0
    nf = nf * row_mask[None]
    return nf.transpose(1, 0, 2).reshape(N, H * O)[None]

@@ -1,0 +1,292 @@
+from contextlib import ExitStack
+import math
+
+import concourse.masks as masks
+import concourse.mybir as mybir
+
+F32 = mybir.dt.float32
+BF16 = mybir.dt.bfloat16
+U32 = mybir.dt.uint32
+U8 = mybir.dt.uint8
+FP8X4 = mybir.dt.float8_e4m3fn_x4
+ALU = mybir.AluOpType
+ACT = mybir.ActivationFunctionType
+AX = mybir.AxisListType
+
+P = 128
+N = 2048
+F = 512
+H = 4
+O = 128
+D = 128
+PACK = 4
+K_PASS = P * PACK
+TILES = N // P
+PASSES = N // K_PASS
+BANK = 512
+CHUNKS = N // BANK
+UNITS = TILES * H
+
+SLOPE = 0.2
+SCALE = 1.0 / math.sqrt(D)
+NO_EDGE = -(2.0**40)
+FLOOR = -(2.0**30)
+TINY = 1.0e-30
+
+FLOPS = 2 * N * F * H * O + 2 * H * N * N * D + 2 * H * N * N * O
+
+
+def tile_gatlayersinglebatch_pa_kernel(tc, h, a, kernel, f_self, f_other, out):
+    nc = tc.nc
+    x_rows = h.rearrange("b (c p e) f -> p (b c) e f", p=P, e=2)
+    adj_rows = a.rearrange("b (c p e) j -> (b c) e p j", p=P, e=2)
+    out_rows = out.rearrange("b (c p e) k -> (b c) e p k", p=P, e=2)
+
+    with ExitStack() as ctx:
+        const = ctx.enter_context(tc.tile_pool(name="const", bufs=1))
+        setup = ctx.enter_context(tc.tile_pool(name="setup", bufs=1))
+        raw = ctx.enter_context(tc.tile_pool(name="raw", bufs=4))
+        junkp = ctx.enter_context(tc.tile_pool(name="junk", bufs=2))
+        adjp = ctx.enter_context(tc.tile_pool(name="adj", bufs=2))
+        tp = ctx.enter_context(tc.tile_pool(name="t", bufs=3))
+        emp = ctx.enter_context(tc.tile_pool(name="em", bufs=2))
+        small = ctx.enter_context(tc.tile_pool(name="small", bufs=3))
+        outp = ctx.enter_context(tc.tile_pool(name="outp", bufs=2))
+        psum_dense = ctx.enter_context(tc.psum_pool(name="psum_dense", bufs=4))
+        psum_tr = ctx.enter_context(tc.psum_pool(name="psum_tr", bufs=2))
+        psum_acc = ctx.enter_context(tc.psum_pool(name="psum_acc", bufs=2))
+
+        ident_bf = const.tile([P, P], BF16)
+        masks.make_identity(nc, ident_bf[:])
+        ident_f32 = const.tile([P, P], F32)
+        masks.make_identity(nc, ident_f32[:])
+
+        fsT = const.tile([P, H, N], BF16)
+        foT = const.tile([P, H, N], BF16)
+        for hd in range(H):
+            fo_raw = raw.tile([P, TILES, D], BF16, tag="fraw")
+            nc.sync.dma_start(out=fo_raw[:], in_=f_other[hd, :, :].rearrange("(t p) d -> p t d", p=P))
+            fs_raw = raw.tile([P, TILES, D], BF16, tag="fraw")
+            nc.sync.dma_start(
+                out=fs_raw[:].rearrange("p (c e) d -> p c e d", e=2),
+                in_=f_self[hd, :, :].rearrange("(c p e) d -> p c e d", p=P, e=2),
+            )
+            for src, dst in ((fo_raw, foT), (fs_raw, fsT)):
+                for blk in range(TILES // 4):
+                    pt = psum_dense.tile([P, 4, P], BF16, tag="dense")
+                    for k in range(4):
+                        nc.tensor.transpose(pt[:, k, :], src[:, 4 * blk + k, :], ident_bf[:])
+                    dst_cols = dst[:, hd, 4 * blk * P : 4 * (blk + 1) * P]
+                    if blk % 2 == 0:
+                        nc.vector.tensor_copy(out=dst_cols, in_=pt[:].rearrange("p k n -> p (k n)"))
+                    else:
+                        nc.scalar.copy(out=dst_cols, in_=pt[:].rearrange("p k n -> p (k n)"))
+
+        k_raw = setup.tile([P, H, PACK, O], BF16)
+        for hd in range(H):
+            nc.sync.dma_start(
+                out=k_raw[:, hd, :, :].rearrange("p (u e) o -> p u e o", u=2),
+                in_=kernel[hd, :, :].rearrange("(u p e) o -> p u e o", u=2, e=2),
+            )
+        k_grp = setup.tile([P, H, O, PACK], BF16, align_bytes=64)
+        nc.vector.tensor_copy(out=k_grp[:], in_=k_raw[:].rearrange("p h t o -> p h o t"))
+        k_codes = setup.tile([P, H * O], U32, align_bytes=64)
+        k_scales = setup.tile([P, H * O], U8, align_bytes=64)
+
+        x_raw = setup.tile([P, TILES // 2, 2, F], BF16)
+        nc.sync.dma_start(out=x_raw[:], in_=x_rows)
+        x_grp = setup.tile([P, TILES * P * PACK], BF16, align_bytes=64)
+        x_grp32 = x_grp[:].bitcast(F32).rearrange("p (t n u) -> p t n u", t=TILES, u=2)
+        absum = const.tile([P, TILES], F32)
+        for pair in range(TILES // 2):
+            xt = psum_tr.tile([P, 2, 2, P], F32, tag="tr")
+            for e in range(2):
+                words = x_raw[:, pair, e, :].bitcast(F32)
+                for u in range(2):
+                    nc.tensor.transpose(xt[:, e, u, :], words[:, u * P : (u + 1) * P], ident_f32[:])
+                junk = junkp.tile([P, F], BF16)
+                nc.scalar.activation(
+                    out=junk[:],
+                    in_=x_raw[:, pair, e, :],
+                    func=ACT.Abs,
+                    accum_out=absum[:, 2 * pair + e : 2 * pair + e + 1],
+                )
+            nc.vector.tensor_copy(
+                out=x_grp32[:, 2 * pair : 2 * pair + 2, :, :], in_=xt[:].rearrange("p t u n -> p t n u")
+            )
+        rowmask = const.tile([P, TILES], F32)
+        nc.vector.tensor_single_scalar(out=rowmask[:], in_=absum[:], scalar=0.0, op=ALU.is_gt)
+
+        nc.vector.quantize_mx(
+            out=k_codes[:].bitcast(FP8X4), scales=k_scales[:], in_=k_grp[:].rearrange("p h o t -> p (h o t)")
+        )
+        x_codes = setup.tile([P, TILES * P], U32, align_bytes=64)
+        x_scales = setup.tile([P, TILES * P], U8, align_bytes=64)
+        for half in range(2):
+            words = slice(half * 1024, (half + 1) * 1024)
+            nc.vector.quantize_mx(
+                out=x_codes[:, words].bitcast(FP8X4),
+                scales=x_scales[:, words],
+                in_=x_grp[:, half * 4096 : (half + 1) * 4096],
+            )
+
+        f_grp = setup.tile([P, PASSES, H, O, PACK], BF16, align_bytes=64)
+        f_codes = const.tile([P, PASSES, H, O], U32, align_bytes=64)
+        f_scales = const.tile([P, PASSES, H, O], U8, align_bytes=64)
+        for g in range(PASSES):
+            for hd in range(H):
+                fb = psum_dense.tile([P, PACK, O], F32, tag="dense")
+                for t in range(PACK):
+                    nodes = slice((PACK * g + t) * P, (PACK * g + t + 1) * P)
+                    nc.tensor.matmul_mx(
+                        out=fb[:, t, :],
+                        lhsT=x_codes[:, nodes].bitcast(FP8X4),
+                        lhsT_scale=x_scales[:, nodes],
+                        rhs=k_codes[:, hd * O : (hd + 1) * O].bitcast(FP8X4),
+                        rhs_scale=k_scales[:, hd * O : (hd + 1) * O],
+                        start=True,
+                        stop=True,
+                    )
+                if hd % 2 == 0:
+                    nc.vector.tensor_copy(out=f_grp[:, g, hd, :, :], in_=fb[:].rearrange("p t o -> p o t"))
+                else:
+                    nc.scalar.copy(out=f_grp[:, g, hd, :, :], in_=fb[:].rearrange("p t o -> p o t"))
+            nc.vector.quantize_mx(
+                out=f_codes[:, g, :, :].rearrange("p h o -> p (h o)").bitcast(FP8X4),
+                scales=f_scales[:, g, :, :].rearrange("p h o -> p (h o)"),
+                in_=f_grp[:, g, :, :, :].rearrange("p h o t -> p (h o t)"),
+            )
+
+        adj_of = {}
+        mask_of = {}
+        banks_of = {}
+        t_of = {}
+        em_of = {}
+        grp_of = {}
+        den_of = {}
+        acc_of = {}
+
+        def load_adj(tile_no):
+            adj_t = adjp.tile([P, N], BF16, tag="adj")
+            nc.sync.dma_start(out=adj_t[:], in_=adj_rows[tile_no // 2, tile_no % 2])
+            adj_of[tile_no] = adj_t
+
+        def make_mask(tile_no):
+            no_edge = adjp.tile([P, N], BF16, tag="mask")
+            nc.vector.tensor_scalar(
+                out=no_edge[:], in0=adj_of[tile_no][:], scalar1=0.0, scalar2=NO_EDGE, op0=ALU.is_equal, op1=ALU.mult
+            )
+            mask_of[tile_no] = no_edge
+
+        def dense(i):
+            tile_no, hd = divmod(i, H)
+            banks = []
+            for q in range(CHUNKS):
+                bank = psum_dense.tile([P, BANK], F32, tag="dense")
+                nc.tensor.matmul(
+                    bank[:],
+                    lhsT=fsT[:, hd, tile_no * P : (tile_no + 1) * P],
+                    rhs=foT[:, hd, q * BANK : (q + 1) * BANK],
+                    start=True,
+                    stop=True,
+                )
+                banks.append(bank)
+            banks_of[i] = banks
+
+        def weigh(i):
+            tile_no = i // H
+            t = tp.tile([P, N], F32, tag="t")
+            for q in range(CHUNKS):
+                cols = slice(q * BANK, (q + 1) * BANK)
+                nc.vector.tensor_tensor(out=t[:, cols], in0=banks_of[i][q][:], in1=adj_of[tile_no][:, cols], op=ALU.mult)
+                nc.gpsimd.tensor_tensor(out=t[:, cols], in0=t[:, cols], in1=mask_of[tile_no][:, cols], op=ALU.add)
+            t_of[i] = t
+
+        def softmax(i):
+            tile_no, hd = divmod(i, H)
+            t = t_of[i]
+            if hd == 0:
+                den = small.tile([P, H], F32, tag="den")
+                den_of[tile_no] = den
+            nc.vector.scalar_tensor_tensor(out=t[:], in0=t[:], scalar=SLOPE, in1=t[:], op0=ALU.mult, op1=ALU.max)
+            top = small.tile([P, 1], F32, tag="top")
+            nc.vector.tensor_reduce(out=top[:], in_=t[:], axis=AX.X, op=ALU.max)
+            shift = small.tile([P, 1], F32, tag="shift")
+            nc.vector.tensor_scalar(
+                out=shift[:], in0=top[:], scalar1=FLOOR, scalar2=-SCALE, op0=ALU.max, op1=ALU.mult
+            )
+            em = emp.tile([P, N], BF16, tag="em")
+            nc.scalar.activation(
+                out=em[:],
+                in_=t[:],
+                func=ACT.Exp,
+                bias=shift[:, 0:1],
+                scale=SCALE,
+                accum_out=den_of[tile_no][:, hd : hd + 1],
+            )
+            em_of[i] = em
+
+        def turn(i):
+            words = em_of[i][:].bitcast(F32)
+            grp = emp.tile([P, N], BF16, tag="grp", align_bytes=64)
+            grp32 = grp[:].bitcast(F32).rearrange("p (g n u) -> p g n u", g=PASSES, u=2)
+            for half in range(2):
+                tr = psum_tr.tile([P, 2, 2, P], F32, tag="tr")
+                for gg in range(2):
+                    for u in range(2):
+                        first = (2 * (2 * half + gg) + u) * P
+                        nc.tensor.transpose(tr[:, gg, u, :], words[:, first : first + P], ident_f32[:])
+                nc.scalar.copy(out=grp32[:, 2 * half : 2 * half + 2, :, :], in_=tr[:].rearrange("p g u n -> p g n u"))
+            grp_of[i] = grp
+
+        def aggregate(i):
+            tile_no, hd = divmod(i, H)
+            codes = emp.tile([P, PASSES * P], U32, tag="codes", align_bytes=64)
+            scales = emp.tile([P, PASSES * P], U8, tag="scales", align_bytes=64)
+            nc.vector.quantize_mx(out=codes[:].bitcast(FP8X4), scales=scales[:], in_=grp_of[i][:])
+            if hd == 0:
+                acc = psum_acc.tile([P, H, O], F32, tag="acc")
+                acc_of[tile_no] = acc
+            for g in range(PASSES):
+                nc.tensor.matmul_mx(
+                    out=acc_of[tile_no][:, hd, :],
+                    lhsT=codes[:, g * P : (g + 1) * P].bitcast(FP8X4),
+                    lhsT_scale=scales[:, g * P : (g + 1) * P],
+                    rhs=f_codes[:, g, hd, :].bitcast(FP8X4),
+                    rhs_scale=f_scales[:, g, hd, :],
+                    start=(g == 0),
+                    stop=(g == PASSES - 1),
+                )
+            if hd == H - 1:
+                gain = small.tile([P, H], F32, tag="gain")
+                nc.vector.tensor_scalar_max(out=gain[:], in0=den_of[tile_no][:], scalar1=TINY)
+                nc.vector.reciprocal(out=gain[:], in_=gain[:])
+                nc.vector.tensor_scalar_mul(out=gain[:], in0=gain[:], scalar1=rowmask[:, tile_no : tile_no + 1])
+                o_sb = outp.tile([P, H, O], F32, tag="o_sb")
+                for k in range(H):
+                    nc.scalar.activation(
+                        out=o_sb[:, k, :], in_=acc_of[tile_no][:, k, :], func=ACT.Relu, scale=gain[:, k : k + 1]
+                    )
+                nc.sync.dma_start(out=out_rows[tile_no // 2, tile_no % 2], in_=o_sb[:].rearrange("p h o -> p (h o)"))
+
+        load_adj(0)
+        make_mask(0)
+        load_adj(1)
+        dense(0)
+        weigh(0)
+        dense(1)
+        for i in range(UNITS):
+            nxt = i + 1
+            if nxt < UNITS:
+                if nxt % H == 0:
+                    make_mask(nxt // H)
+                    if nxt // H + 1 < TILES:
+                        load_adj(nxt // H + 1)
+                weigh(nxt)
+            if i + 2 < UNITS:
+                dense(i + 2)
+            softmax(i)
+            if i >= 1:
+                aggregate(i - 1)
+            turn(i)
+        aggregate(UNITS - 1)

@@ -48,6 +48,7 @@ def tile_gatlayersinglebatch_pa_kernel(tc, h, a, kernel, f_self, f_other, out):
         raw = ctx.enter_context(tc.tile_pool(name="raw", bufs=4))
         junkp = ctx.enter_context(tc.tile_pool(name="junk", bufs=2))
         adjp = ctx.enter_context(tc.tile_pool(name="adj", bufs=2))
+        maskp = ctx.enter_context(tc.tile_pool(name="maskp", bufs=2))
         tp = ctx.enter_context(tc.tile_pool(name="t", bufs=3))
         emp = ctx.enter_context(tc.tile_pool(name="em", bufs=2))
         small = ctx.enter_context(tc.tile_pool(name="small", bufs=3))
@@ -159,6 +160,7 @@ def tile_gatlayersinglebatch_pa_kernel(tc, h, a, kernel, f_self, f_other, out):
 
         adj_of = {}
         mask_of = {}
+        weight_of = {}
         banks_of = {}
         t_of = {}
         em_of = {}
@@ -172,11 +174,18 @@ def tile_gatlayersinglebatch_pa_kernel(tc, h, a, kernel, f_self, f_other, out):
             adj_of[tile_no] = adj_t
 
         def make_mask(tile_no):
-            no_edge = adjp.tile([P, N], BF16, tag="mask")
-            nc.vector.tensor_scalar(
-                out=no_edge[:], in0=adj_of[tile_no][:], scalar1=0.0, scalar2=NO_EDGE, op0=ALU.is_equal, op1=ALU.mult
-            )
-            mask_of[tile_no] = no_edge
+            is_zero = adjp.tile([P, N], BF16, tag="is_zero")
+            nc.vector.tensor_single_scalar(out=is_zero[:], in_=adj_of[tile_no][:], scalar=0.0, op=ALU.is_equal)
+            weight = adjp.tile([P, N], BF16, tag="weight")
+            nc.vector.tensor_tensor(out=weight[:], in0=adj_of[tile_no][:], in1=is_zero[:], op=ALU.add)
+            weight_of[tile_no] = weight
+            maskT = maskp.tile([P, TILES, P], F32, tag="maskT")
+            for blk in range(TILES // 4):
+                zt = psum_tr.tile([P, 4, P], BF16, tag="tr")
+                for k in range(4):
+                    nc.tensor.transpose(zt[:, k, :], is_zero[:, (4 * blk + k) * P : (4 * blk + k + 1) * P], ident_bf[:])
+                nc.scalar.activation(out=maskT[:, 4 * blk : 4 * blk + 4, :], in_=zt[:], func=ACT.Copy, scale=NO_EDGE)
+            mask_of[tile_no] = maskT
 
         def dense(i):
             tile_no, hd = divmod(i, H)
@@ -188,8 +197,17 @@ def tile_gatlayersinglebatch_pa_kernel(tc, h, a, kernel, f_self, f_other, out):
                     lhsT=fsT[:, hd, tile_no * P : (tile_no + 1) * P],
                     rhs=foT[:, hd, q * BANK : (q + 1) * BANK],
                     start=True,
-                    stop=True,
+                    stop=False,
                 )
+                for k in range(4):
+                    nc.tensor.matmul(
+                        bank[:, k * P : (k + 1) * P],
+                        lhsT=mask_of[tile_no][:, 4 * q + k, :],
+                        rhs=ident_f32[:],
+                        is_transpose=True,
+                        start=False,
+                        stop=(k == 3),
+                    )
                 banks.append(bank)
             banks_of[i] = banks
 
@@ -198,8 +216,9 @@ def tile_gatlayersinglebatch_pa_kernel(tc, h, a, kernel, f_self, f_other, out):
             t = tp.tile([P, N], F32, tag="t")
             for q in range(CHUNKS):
                 cols = slice(q * BANK, (q + 1) * BANK)
-                nc.vector.tensor_tensor(out=t[:, cols], in0=banks_of[i][q][:], in1=adj_of[tile_no][:, cols], op=ALU.mult)
-                nc.gpsimd.tensor_tensor(out=t[:, cols], in0=t[:, cols], in1=mask_of[tile_no][:, cols], op=ALU.add)
+                nc.vector.tensor_tensor(
+                    out=t[:, cols], in0=banks_of[i][q][:], in1=weight_of[tile_no][:, cols], op=ALU.mult
+                )
             t_of[i] = t
 
         def softmax(i):
@@ -276,14 +295,13 @@ def tile_gatlayersinglebatch_pa_kernel(tc, h, a, kernel, f_self, f_other, out):
         weigh(0)
         dense(1)
         for i in range(UNITS):
-            nxt = i + 1
-            if nxt < UNITS:
-                if nxt % H == 0:
-                    make_mask(nxt // H)
-                    if nxt // H + 1 < TILES:
-                        load_adj(nxt // H + 1)
-                weigh(nxt)
+            if i + 1 < UNITS:
+                weigh(i + 1)
             if i + 2 < UNITS:
+                if (i + 2) % H == 0:
+                    make_mask((i + 2) // H)
+                    if (i + 2) // H + 1 < TILES:
+                        load_adj((i + 2) // H + 1)
                 dense(i + 2)
             softmax(i)
             if i >= 1:

@@ -29,7 +29,8 @@ UNITS = TILES * H
 
 SLOPE = 0.2
 SCALE = 1.0 / math.sqrt(D)
-NO_EDGE = -(2.0**40)
+NO_EDGE = -(2.0**100)
+LEAST_WEIGHT = 2.0**-60
 FLOOR = -(2.0**30)
 TINY = 1.0e-30
 
@@ -50,6 +51,7 @@ def tile_gatlayersinglebatch_pa_kernel(tc, h, a, kernel, f_self, f_other, out):
         adjp = ctx.enter_context(tc.tile_pool(name="adj", bufs=2))
         maskp = ctx.enter_context(tc.tile_pool(name="maskp", bufs=2))
         tp = ctx.enter_context(tc.tile_pool(name="t", bufs=3))
+        zp = ctx.enter_context(tc.tile_pool(name="z", bufs=3))
         emp = ctx.enter_context(tc.tile_pool(name="em", bufs=2))
         small = ctx.enter_context(tc.tile_pool(name="small", bufs=3))
         outp = ctx.enter_context(tc.tile_pool(name="outp", bufs=2))
@@ -96,7 +98,7 @@ def tile_gatlayersinglebatch_pa_kernel(tc, h, a, kernel, f_self, f_other, out):
 
         x_raw = setup.tile([P, TILES // 2, 2, F], BF16)
         nc.sync.dma_start(out=x_raw[:], in_=x_rows)
-        x_grp = setup.tile([P, TILES * P * PACK], BF16, align_bytes=64)
+        x_grp = setup.tile([P, TILES * P * PACK], BF16, tag="grouped", align_bytes=64)
         x_grp32 = x_grp[:].bitcast(F32).rearrange("p (t n u) -> p t n u", t=TILES, u=2)
         absum = const.tile([P, TILES], F32)
         for pair in range(TILES // 2):
@@ -131,7 +133,7 @@ def tile_gatlayersinglebatch_pa_kernel(tc, h, a, kernel, f_self, f_other, out):
                 in_=x_grp[:, half * 4096 : (half + 1) * 4096],
             )
 
-        f_grp = setup.tile([P, PASSES, H, O, PACK], BF16, align_bytes=64)
+        f_grp = setup.tile([P, PASSES, H, O, PACK], BF16, tag="grouped", align_bytes=64)
         f_codes = const.tile([P, PASSES, H, O], U32, align_bytes=64)
         f_scales = const.tile([P, PASSES, H, O], U8, align_bytes=64)
         for g in range(PASSES):
@@ -162,7 +164,8 @@ def tile_gatlayersinglebatch_pa_kernel(tc, h, a, kernel, f_self, f_other, out):
         mask_of = {}
         weight_of = {}
         banks_of = {}
-        t_of = {}
+        z_of = {}
+        shift_of = {}
         em_of = {}
         grp_of = {}
         den_of = {}
@@ -177,7 +180,7 @@ def tile_gatlayersinglebatch_pa_kernel(tc, h, a, kernel, f_self, f_other, out):
             is_zero = adjp.tile([P, N], BF16, tag="is_zero")
             nc.vector.tensor_single_scalar(out=is_zero[:], in_=adj_of[tile_no][:], scalar=0.0, op=ALU.is_equal)
             weight = adjp.tile([P, N], BF16, tag="weight")
-            nc.vector.tensor_tensor(out=weight[:], in0=adj_of[tile_no][:], in1=is_zero[:], op=ALU.add)
+            nc.vector.tensor_scalar_max(out=weight[:], in0=adj_of[tile_no][:], scalar1=LEAST_WEIGHT)
             weight_of[tile_no] = weight
             maskT = maskp.tile([P, TILES, P], F32, tag="maskT")
             for blk in range(TILES // 4):
@@ -219,27 +222,33 @@ def tile_gatlayersinglebatch_pa_kernel(tc, h, a, kernel, f_self, f_other, out):
                 nc.vector.tensor_tensor(
                     out=t[:, cols], in0=banks_of[i][q][:], in1=weight_of[tile_no][:, cols], op=ALU.mult
                 )
-            t_of[i] = t
+            z = zp.tile([P, N], F32, tag="z")
+            nc.scalar.activation(out=z[:], in_=t[:], func=ACT.Relu, scale=-(1.0 - SLOPE))
+            for q in range(CHUNKS):
+                cols = slice(q * BANK, (q + 1) * BANK)
+                nc.gpsimd.tensor_tensor(out=z[:, cols], in0=t[:, cols], in1=z[:, cols], op=ALU.add)
+            z_of[i] = z
+            top = small.tile([P, 1], F32, tag="top")
+            nc.vector.tensor_reduce(out=top[:], in_=t[:], axis=AX.X, op=ALU.max)
+            bent = small.tile([P, 1], F32, tag="bent")
+            nc.vector.scalar_tensor_tensor(out=bent[:], in0=top[:], scalar=SLOPE, in1=top[:], op0=ALU.mult, op1=ALU.max)
+            shift = small.tile([P, 1], F32, tag="shift")
+            nc.vector.tensor_scalar(
+                out=shift[:], in0=bent[:], scalar1=FLOOR, scalar2=-SCALE, op0=ALU.max, op1=ALU.mult
+            )
+            shift_of[i] = shift
 
         def softmax(i):
             tile_no, hd = divmod(i, H)
-            t = t_of[i]
             if hd == 0:
                 den = small.tile([P, H], F32, tag="den")
                 den_of[tile_no] = den
-            nc.vector.scalar_tensor_tensor(out=t[:], in0=t[:], scalar=SLOPE, in1=t[:], op0=ALU.mult, op1=ALU.max)
-            top = small.tile([P, 1], F32, tag="top")
-            nc.vector.tensor_reduce(out=top[:], in_=t[:], axis=AX.X, op=ALU.max)
-            shift = small.tile([P, 1], F32, tag="shift")
-            nc.vector.tensor_scalar(
-                out=shift[:], in0=top[:], scalar1=FLOOR, scalar2=-SCALE, op0=ALU.max, op1=ALU.mult
-            )
             em = emp.tile([P, N], BF16, tag="em")
             nc.scalar.activation(
                 out=em[:],
-                in_=t[:],
+                in_=z_of[i][:],
                 func=ACT.Exp,
-                bias=shift[:, 0:1],
+                bias=shift_of[i][:, 0:1],
                 scale=SCALE,
                 accum_out=den_of[tile_no][:, hd : hd + 1],
             )
@@ -288,23 +297,26 @@ def tile_gatlayersinglebatch_pa_kernel(tc, h, a, kernel, f_self, f_other, out):
                     )
                 nc.sync.dma_start(out=out_rows[tile_no // 2, tile_no % 2], in_=o_sb[:].rearrange("p h o -> p (h o)"))
 
+        def prepare(tile_no):
+            make_mask(tile_no)
+            if tile_no + 1 < TILES:
+                load_adj(tile_no + 1)
+
         load_adj(0)
-        make_mask(0)
-        load_adj(1)
+        prepare(0)
         dense(0)
         weigh(0)
         dense(1)
-        for i in range(UNITS):
-            if i + 1 < UNITS:
-                weigh(i + 1)
-            if i + 2 < UNITS:
-                if (i + 2) % H == 0:
-                    make_mask((i + 2) // H)
-                    if (i + 2) // H + 1 < TILES:
-                        load_adj((i + 2) // H + 1)
-                dense(i + 2)
-            softmax(i)
-            if i >= 1:
-                aggregate(i - 1)
-            turn(i)
-        aggregate(UNITS - 1)
+        for step in range(UNITS + 2):
+            if 1 <= step <= UNITS:
+                softmax(step - 1)
+            if step + 1 < UNITS:
+                weigh(step + 1)
+            if step + 2 < UNITS:
+                if (step + 2) % H == 0:
+                    prepare((step + 2) // H)
+                dense(step + 2)
+            if 1 <= step <= UNITS:
+                turn(step - 1)
+            if step >= 2:
+                aggregate(step - 2)

@@ -26,6 +26,7 @@ PASSES = N // K_PASS
 BANK = 512
 CHUNKS = N // BANK
 UNITS = TILES * H
+VECTOR_CHUNKS = 1
 
 SLOPE = 0.2
 SCALE = 1.0 / math.sqrt(D)
@@ -223,10 +224,15 @@ def tile_gatlayersinglebatch_pa_kernel(tc, h, a, kernel, f_self, f_other, out):
                     out=t[:, cols], in0=banks_of[i][q][:], in1=weight_of[tile_no][:, cols], op=ALU.mult
                 )
             z = zp.tile([P, N], F32, tag="z")
-            nc.scalar.activation(out=z[:], in_=t[:], func=ACT.Relu, scale=-(1.0 - SLOPE))
-            for q in range(CHUNKS):
+            own = slice(0, VECTOR_CHUNKS * BANK)
+            rest = slice(VECTOR_CHUNKS * BANK, N)
+            nc.scalar.activation(out=z[:, rest], in_=t[:, rest], func=ACT.Relu, scale=-(1.0 - SLOPE))
+            for q in range(VECTOR_CHUNKS, CHUNKS):
                 cols = slice(q * BANK, (q + 1) * BANK)
                 nc.gpsimd.tensor_tensor(out=z[:, cols], in0=t[:, cols], in1=z[:, cols], op=ALU.add)
+            nc.vector.scalar_tensor_tensor(
+                out=z[:, own], in0=t[:, own], scalar=SLOPE, in1=t[:, own], op0=ALU.mult, op1=ALU.max
+            )
             z_of[i] = z
             top = small.tile([P, 1], F32, tag="top")
             nc.vector.tensor_reduce(out=top[:], in_=t[:], axis=AX.X, op=ALU.max)

@@ -26,11 +26,11 @@ PASSES = N // K_PASS
 BANK = 512
 CHUNKS = N // BANK
 UNITS = TILES * H
-VECTOR_CHUNKS = 1
 
 SLOPE = 0.2
 SCALE = 1.0 / math.sqrt(D)
-NO_EDGE = -(2.0**100)
+NO_EDGE_LOG = 69.0
+EDGE_SLOPE = 2.0**112
 LEAST_WEIGHT = 2.0**-60
 FLOOR = -(2.0**30)
 TINY = 1.0e-30
@@ -49,7 +49,7 @@ def tile_gatlayersinglebatch_pa_kernel(tc, h, a, kernel, f_self, f_other, out):
         setup = ctx.enter_context(tc.tile_pool(name="setup", bufs=1))
         raw = ctx.enter_context(tc.tile_pool(name="raw", bufs=4))
         junkp = ctx.enter_context(tc.tile_pool(name="junk", bufs=2))
-        adjp = ctx.enter_context(tc.tile_pool(name="adj", bufs=2))
+        adjp = ctx.enter_context(tc.tile_pool(name="adj", bufs=3))
         maskp = ctx.enter_context(tc.tile_pool(name="maskp", bufs=2))
         tp = ctx.enter_context(tc.tile_pool(name="t", bufs=3))
         zp = ctx.enter_context(tc.tile_pool(name="z", bufs=3))
@@ -81,8 +81,8 @@ def tile_gatlayersinglebatch_pa_kernel(tc, h, a, kernel, f_self, f_other, out):
                     for k in range(4):
                         nc.tensor.transpose(pt[:, k, :], src[:, 4 * blk + k, :], ident_bf[:])
                     dst_cols = dst[:, hd, 4 * blk * P : 4 * (blk + 1) * P]
-                    if blk % 2 == 0:
-                        nc.vector.tensor_copy(out=dst_cols, in_=pt[:].rearrange("p k n -> p (k n)"))
+                    if dst is fsT:
+                        nc.vector.tensor_scalar_mul(out=dst_cols, in0=pt[:].rearrange("p k n -> p (k n)"), scalar1=-1.0)
                     else:
                         nc.scalar.copy(out=dst_cols, in_=pt[:].rearrange("p k n -> p (k n)"))
 
@@ -161,15 +161,24 @@ def tile_gatlayersinglebatch_pa_kernel(tc, h, a, kernel, f_self, f_other, out):
                 in_=f_grp[:, g, :, :, :].rearrange("p h o t -> p (h o t)"),
             )
 
+        log_bias = const.tile([P, 1], F32)
+        nc.vector.memset(log_bias[:], NO_EDGE_LOG)
+
         adj_of = {}
         mask_of = {}
         weight_of = {}
         banks_of = {}
+        t_of = {}
         z_of = {}
+        top_of = {}
+        bent_of = {}
         shift_of = {}
         em_of = {}
+        tr_of = {}
         grp_of = {}
+        codes_of = {}
         den_of = {}
+        gain_of = {}
         acc_of = {}
 
         def load_adj(tile_no):
@@ -177,74 +186,90 @@ def tile_gatlayersinglebatch_pa_kernel(tc, h, a, kernel, f_self, f_other, out):
             nc.sync.dma_start(out=adj_t[:], in_=adj_rows[tile_no // 2, tile_no % 2])
             adj_of[tile_no] = adj_t
 
-        def make_mask(tile_no):
-            is_zero = adjp.tile([P, N], BF16, tag="is_zero")
-            nc.vector.tensor_single_scalar(out=is_zero[:], in_=adj_of[tile_no][:], scalar=0.0, op=ALU.is_equal)
+        def make_weight(tile_no):
             weight = adjp.tile([P, N], BF16, tag="weight")
-            nc.vector.tensor_scalar_max(out=weight[:], in0=adj_of[tile_no][:], scalar1=LEAST_WEIGHT)
-            weight_of[tile_no] = weight
-            maskT = maskp.tile([P, TILES, P], F32, tag="maskT")
-            for blk in range(TILES // 4):
-                zt = psum_tr.tile([P, 4, P], BF16, tag="tr")
-                for k in range(4):
-                    nc.tensor.transpose(zt[:, k, :], is_zero[:, (4 * blk + k) * P : (4 * blk + k + 1) * P], ident_bf[:])
-                nc.scalar.activation(out=maskT[:, 4 * blk : 4 * blk + 4, :], in_=zt[:], func=ACT.Copy, scale=NO_EDGE)
-            mask_of[tile_no] = maskT
-
-        def dense(i):
-            tile_no, hd = divmod(i, H)
-            banks = []
-            for q in range(CHUNKS):
-                bank = psum_dense.tile([P, BANK], F32, tag="dense")
-                nc.tensor.matmul(
-                    bank[:],
-                    lhsT=fsT[:, hd, tile_no * P : (tile_no + 1) * P],
-                    rhs=foT[:, hd, q * BANK : (q + 1) * BANK],
-                    start=True,
-                    stop=False,
-                )
-                for k in range(4):
-                    nc.tensor.matmul(
-                        bank[:, k * P : (k + 1) * P],
-                        lhsT=mask_of[tile_no][:, 4 * q + k, :],
-                        rhs=ident_f32[:],
-                        is_transpose=True,
-                        start=False,
-                        stop=(k == 3),
-                    )
-                banks.append(bank)
-            banks_of[i] = banks
-
-        def weigh(i):
-            tile_no = i // H
-            t = tp.tile([P, N], F32, tag="t")
-            for q in range(CHUNKS):
-                cols = slice(q * BANK, (q + 1) * BANK)
-                nc.vector.tensor_tensor(
-                    out=t[:, cols], in0=banks_of[i][q][:], in1=weight_of[tile_no][:, cols], op=ALU.mult
-                )
-            z = zp.tile([P, N], F32, tag="z")
-            own = slice(0, VECTOR_CHUNKS * BANK)
-            rest = slice(VECTOR_CHUNKS * BANK, N)
-            nc.scalar.activation(out=z[:, rest], in_=t[:, rest], func=ACT.Relu, scale=-(1.0 - SLOPE))
-            for q in range(VECTOR_CHUNKS, CHUNKS):
-                cols = slice(q * BANK, (q + 1) * BANK)
-                nc.gpsimd.tensor_tensor(out=z[:, cols], in0=t[:, cols], in1=z[:, cols], op=ALU.add)
-            nc.vector.scalar_tensor_tensor(
-                out=z[:, own], in0=t[:, own], scalar=SLOPE, in1=t[:, own], op0=ALU.mult, op1=ALU.max
+            nc.vector.tensor_scalar(
+                out=weight[:], in0=adj_of[tile_no][:], scalar1=-1.0, scalar2=-LEAST_WEIGHT, op0=ALU.mult, op1=ALU.min
             )
-            z_of[i] = z
+            weight_of[tile_no] = weight
+
+        def mask_part(tile_no, blk):
+            if blk == 0:
+                maskT = maskp.tile([P, TILES, P], F32, tag="maskT")
+                mask_of[tile_no] = maskT
+            adj_t = adj_of[tile_no]
+            zt = psum_tr.tile([P, 4, P], BF16, tag="tr")
+            for k in range(4):
+                nc.tensor.transpose(zt[:, k, :], adj_t[:, (4 * blk + k) * P : (4 * blk + k + 1) * P], ident_bf[:])
+            nc.scalar.activation(
+                out=mask_of[tile_no][:, 4 * blk : 4 * blk + 4, :],
+                in_=zt[:],
+                func=ACT.Exp,
+                bias=log_bias[:, 0:1],
+                scale=-EDGE_SLOPE,
+            )
+
+        def dense(i, q):
+            tile_no, hd = divmod(i, H)
+            bank = psum_dense.tile([P, BANK], F32, tag="dense")
+            nc.tensor.matmul(
+                bank[:],
+                lhsT=fsT[:, hd, tile_no * P : (tile_no + 1) * P],
+                rhs=foT[:, hd, q * BANK : (q + 1) * BANK],
+                start=True,
+                stop=False,
+            )
+            for k in range(4):
+                nc.tensor.matmul(
+                    bank[:, k * P : (k + 1) * P],
+                    lhsT=mask_of[tile_no][:, 4 * q + k, :],
+                    rhs=ident_f32[:],
+                    is_transpose=True,
+                    start=False,
+                    stop=(k == 3),
+                )
+            banks_of[i, q] = bank
+
+        def weigh(i, q):
+            if q == 0:
+                t = tp.tile([P, N], F32, tag="t")
+                t_of[i] = t
+            cols = slice(q * BANK, (q + 1) * BANK)
+            nc.vector.tensor_tensor(
+                out=t_of[i][:, cols], in0=banks_of[i, q][:], in1=weight_of[i // H][:, cols], op=ALU.mult
+            )
+
+        def bend(i, q):
+            if q == 0:
+                z = zp.tile([P, N], F32, tag="z")
+                z_of[i] = z
+            cols = slice(q * BANK, (q + 1) * BANK)
+            t = t_of[i]
+            z = z_of[i]
+            nc.scalar.activation(out=z[:, cols], in_=t[:, cols], func=ACT.Relu, scale=-(1.0 - SLOPE))
+            nc.gpsimd.tensor_tensor(out=z[:, cols], in0=t[:, cols], in1=z[:, cols], op=ALU.add)
+
+        def row_max(i):
             top = small.tile([P, 1], F32, tag="top")
-            nc.vector.tensor_reduce(out=top[:], in_=t[:], axis=AX.X, op=ALU.max)
+            nc.vector.tensor_reduce(out=top[:], in_=t_of[i][:], axis=AX.X, op=ALU.max)
+            top_of[i] = top
+
+        def bend_max(i):
+            top = top_of[i]
             bent = small.tile([P, 1], F32, tag="bent")
-            nc.vector.scalar_tensor_tensor(out=bent[:], in0=top[:], scalar=SLOPE, in1=top[:], op0=ALU.mult, op1=ALU.max)
+            nc.vector.tensor_scalar(
+                out=bent[:], in0=top[:], scalar1=SLOPE, scalar2=top[:, 0:1], op0=ALU.mult, op1=ALU.max
+            )
+            bent_of[i] = bent
+
+        def shift_max(i):
             shift = small.tile([P, 1], F32, tag="shift")
             nc.vector.tensor_scalar(
-                out=shift[:], in0=bent[:], scalar1=FLOOR, scalar2=-SCALE, op0=ALU.max, op1=ALU.mult
+                out=shift[:], in0=bent_of[i][:], scalar1=FLOOR, scalar2=-SCALE, op0=ALU.max, op1=ALU.mult
             )
             shift_of[i] = shift
 
-        def softmax(i):
+        def exponential(i):
             tile_no, hd = divmod(i, H)
             if hd == 0:
                 den = small.tile([P, H], F32, tag="den")
@@ -262,22 +287,35 @@ def tile_gatlayersinglebatch_pa_kernel(tc, h, a, kernel, f_self, f_other, out):
 
         def turn(i):
             words = em_of[i][:].bitcast(F32)
-            grp = emp.tile([P, N], BF16, tag="grp", align_bytes=64)
-            grp32 = grp[:].bitcast(F32).rearrange("p (g n u) -> p g n u", g=PASSES, u=2)
             for half in range(2):
                 tr = psum_tr.tile([P, 2, 2, P], F32, tag="tr")
                 for gg in range(2):
                     for u in range(2):
                         first = (2 * (2 * half + gg) + u) * P
                         nc.tensor.transpose(tr[:, gg, u, :], words[:, first : first + P], ident_f32[:])
-                nc.scalar.copy(out=grp32[:, 2 * half : 2 * half + 2, :, :], in_=tr[:].rearrange("p g u n -> p g n u"))
-            grp_of[i] = grp
+                tr_of[i, half] = tr
 
-        def aggregate(i):
-            tile_no, hd = divmod(i, H)
+        def group(i, half):
+            if half == 0:
+                grp = emp.tile([P, N], BF16, tag="grp", align_bytes=64)
+                grp_of[i] = grp
+            grp32 = grp_of[i][:].bitcast(F32).rearrange("p (g n u) -> p g n u", g=PASSES, u=2)
+            dst = grp32[:, 2 * half : 2 * half + 2, :, :]
+            src = tr_of[i, half][:].rearrange("p g u n -> p g n u")
+            if half == 0:
+                nc.scalar.copy(out=dst, in_=src)
+            else:
+                nc.vector.tensor_copy(out=dst, in_=src)
+
+        def quantise(i):
             codes = emp.tile([P, PASSES * P], U32, tag="codes", align_bytes=64)
             scales = emp.tile([P, PASSES * P], U8, tag="scales", align_bytes=64)
             nc.vector.quantize_mx(out=codes[:].bitcast(FP8X4), scales=scales[:], in_=grp_of[i][:])
+            codes_of[i] = (codes, scales)
+
+        def aggregate(i):
+            tile_no, hd = divmod(i, H)
+            codes, scales = codes_of[i]
             if hd == 0:
                 acc = psum_acc.tile([P, H, O], F32, tag="acc")
                 acc_of[tile_no] = acc
@@ -291,38 +329,78 @@ def tile_gatlayersinglebatch_pa_kernel(tc, h, a, kernel, f_self, f_other, out):
                     start=(g == 0),
                     stop=(g == PASSES - 1),
                 )
-            if hd == H - 1:
-                gain = small.tile([P, H], F32, tag="gain")
-                nc.vector.tensor_scalar_max(out=gain[:], in0=den_of[tile_no][:], scalar1=TINY)
-                nc.vector.reciprocal(out=gain[:], in_=gain[:])
-                nc.vector.tensor_scalar_mul(out=gain[:], in0=gain[:], scalar1=rowmask[:, tile_no : tile_no + 1])
-                o_sb = outp.tile([P, H, O], F32, tag="o_sb")
-                for k in range(H):
-                    nc.scalar.activation(
-                        out=o_sb[:, k, :], in_=acc_of[tile_no][:, k, :], func=ACT.Relu, scale=gain[:, k : k + 1]
-                    )
-                nc.sync.dma_start(out=out_rows[tile_no // 2, tile_no % 2], in_=o_sb[:].rearrange("p h o -> p (h o)"))
 
-        def prepare(tile_no):
-            make_mask(tile_no)
-            if tile_no + 1 < TILES:
-                load_adj(tile_no + 1)
+        def gain_step(tile_no, part):
+            if part == 0:
+                gain = small.tile([P, H], F32, tag="gain")
+                gain_of[tile_no] = gain
+                nc.vector.tensor_scalar_max(out=gain[:], in0=den_of[tile_no][:], scalar1=TINY)
+            elif part == 1:
+                nc.vector.reciprocal(out=gain_of[tile_no][:], in_=gain_of[tile_no][:])
+            else:
+                nc.vector.tensor_scalar_mul(
+                    out=gain_of[tile_no][:], in0=gain_of[tile_no][:], scalar1=rowmask[:, tile_no : tile_no + 1]
+                )
+
+        def finish(tile_no):
+            o_sb = outp.tile([P, H, O], F32, tag="o_sb")
+            for k in range(H):
+                nc.scalar.activation(
+                    out=o_sb[:, k, :],
+                    in_=acc_of[tile_no][:, k, :],
+                    func=ACT.Relu,
+                    scale=gain_of[tile_no][:, k : k + 1],
+                )
+            nc.sync.dma_start(out=out_rows[tile_no // 2, tile_no % 2], in_=o_sb[:].rearrange("p h o -> p (h o)"))
 
         load_adj(0)
-        prepare(0)
-        dense(0)
-        weigh(0)
-        dense(1)
-        for step in range(UNITS + 2):
-            if 1 <= step <= UNITS:
-                softmax(step - 1)
-            if step + 1 < UNITS:
-                weigh(step + 1)
-            if step + 2 < UNITS:
-                if (step + 2) % H == 0:
-                    prepare((step + 2) // H)
-                dense(step + 2)
-            if 1 <= step <= UNITS:
-                turn(step - 1)
-            if step >= 2:
-                aggregate(step - 2)
+        load_adj(1)
+        make_weight(0)
+        for blk in range(TILES // 4):
+            mask_part(0, blk)
+        engines = {mybir.EngineType.PE, mybir.EngineType.DVE, mybir.EngineType.Activation, mybir.EngineType.Pool}
+        with tc.manual_schedule(engines=engines):
+            for q in range(CHUNKS):
+                dense(0, q)
+            for step in range(UNITS + 4):
+                tile_no, hd = divmod(step, H)
+                live = step < UNITS
+                old = step - 3
+                if 0 <= step - 2 < UNITS:
+                    group(step - 2, 0)
+                if live:
+                    weigh(step, 0)
+                    bend(step, 0)
+                if 0 <= old < UNITS:
+                    quantise(old)
+                if live and hd == 2 and tile_no + 1 < TILES:
+                    make_weight(tile_no + 1)
+                if step + 1 < UNITS:
+                    dense(step + 1, 0)
+                if 0 <= old < UNITS:
+                    aggregate(old)
+                if live and tile_no + 1 < TILES:
+                    mask_part(tile_no + 1, hd)
+                if hd == 0 and tile_no + 2 < TILES:
+                    load_adj(tile_no + 2)
+                for q in range(1, CHUNKS):
+                    if live:
+                        weigh(step, q)
+                        bend(step, q)
+                    if step + 1 < UNITS:
+                        dense(step + 1, q)
+                    if q == 1 and 0 <= step - 1 < UNITS:
+                        bend_max(step - 1)
+                    if q == 2 and 0 <= step - 1 < UNITS:
+                        shift_max(step - 1)
+                    if hd == 1 and step >= H + 1:
+                        gain_step(tile_no - 1, q - 1)
+                if 0 <= step - 2 < UNITS:
+                    group(step - 2, 1)
+                if live:
+                    row_max(step)
+                if 0 <= step - 1 < UNITS:
+                    exponential(step - 1)
+                    turn(step - 1)
+                if hd == 2 and step >= H + 2:
+                    finish(tile_no - 1)

@@ -51,14 +51,15 @@ def tile_gatlayersinglebatch_pa_kernel(tc, h, a, kernel, f_self, f_other, out):
         junkp = ctx.enter_context(tc.tile_pool(name="junk", bufs=2))
         adjp = ctx.enter_context(tc.tile_pool(name="adj", bufs=3))
         maskp = ctx.enter_context(tc.tile_pool(name="maskp", bufs=2))
-        tp = ctx.enter_context(tc.tile_pool(name="t", bufs=3))
-        zp = ctx.enter_context(tc.tile_pool(name="z", bufs=3))
-        emp = ctx.enter_context(tc.tile_pool(name="em", bufs=2))
+        tp = ctx.enter_context(tc.tile_pool(name="t", bufs=2))
+        zp = ctx.enter_context(tc.tile_pool(name="z", bufs=2))
+        emp = ctx.enter_context(tc.tile_pool(name="em", bufs=3))
         small = ctx.enter_context(tc.tile_pool(name="small", bufs=3))
         outp = ctx.enter_context(tc.tile_pool(name="outp", bufs=2))
         psum_dense = ctx.enter_context(tc.psum_pool(name="psum_dense", bufs=4))
         psum_tr = ctx.enter_context(tc.psum_pool(name="psum_tr", bufs=2))
-        psum_acc = ctx.enter_context(tc.psum_pool(name="psum_acc", bufs=2))
+        psum_mask = ctx.enter_context(tc.psum_pool(name="psum_mask", bufs=1))
+        psum_acc = ctx.enter_context(tc.psum_pool(name="psum_acc", bufs=1))
 
         ident_bf = const.tile([P, P], BF16)
         masks.make_identity(nc, ident_bf[:])
@@ -198,7 +199,7 @@ def tile_gatlayersinglebatch_pa_kernel(tc, h, a, kernel, f_self, f_other, out):
                 maskT = maskp.tile([P, TILES, P], F32, tag="maskT")
                 mask_of[tile_no] = maskT
             adj_t = adj_of[tile_no]
-            zt = psum_tr.tile([P, 4, P], BF16, tag="tr")
+            zt = psum_mask.tile([P, 4, P], BF16, tag="zt")
             for k in range(4):
                 nc.tensor.transpose(zt[:, k, :], adj_t[:, (4 * blk + k) * P : (4 * blk + k + 1) * P], ident_bf[:])
             nc.scalar.activation(
@@ -239,11 +240,11 @@ def tile_gatlayersinglebatch_pa_kernel(tc, h, a, kernel, f_self, f_other, out):
                 out=t_of[i][:, cols], in0=banks_of[i, q][:], in1=weight_of[i // H][:, cols], op=ALU.mult
             )
 
-        def bend(i, q):
-            if q == 0:
+        def bend(i, first, last):
+            if first == 0:
                 z = zp.tile([P, N], F32, tag="z")
                 z_of[i] = z
-            cols = slice(q * BANK, (q + 1) * BANK)
+            cols = slice(first * BANK, last * BANK)
             t = t_of[i]
             z = z_of[i]
             nc.scalar.activation(out=z[:, cols], in_=t[:, cols], func=ACT.Relu, scale=-(1.0 - SLOPE))
@@ -362,45 +363,42 @@ def tile_gatlayersinglebatch_pa_kernel(tc, h, a, kernel, f_self, f_other, out):
         with tc.manual_schedule(engines=engines):
             for q in range(CHUNKS):
                 dense(0, q)
-            for step in range(UNITS + 4):
+            for step in range(UNITS + 5):
                 tile_no, hd = divmod(step, H)
                 live = step < UNITS
-                old = step - 3
-                if 0 <= step - 2 < UNITS:
-                    group(step - 2, 0)
-                if live:
-                    weigh(step, 0)
-                    bend(step, 0)
-                if 0 <= old < UNITS:
-                    quantise(old)
-                if live and hd == 2 and tile_no + 1 < TILES:
-                    make_weight(tile_no + 1)
-                if step + 1 < UNITS:
-                    dense(step + 1, 0)
-                if 0 <= old < UNITS:
-                    aggregate(old)
-                if live and tile_no + 1 < TILES:
-                    mask_part(tile_no + 1, hd)
                 if hd == 0 and tile_no + 2 < TILES:
                     load_adj(tile_no + 2)
-                for q in range(1, CHUNKS):
+                for q in range(CHUNKS):
                     if live:
                         weigh(step, q)
-                        bend(step, q)
                     if step + 1 < UNITS:
                         dense(step + 1, q)
+                    if q == 0:
+                        if 0 <= step - 5:
+                            aggregate(step - 5)
+                        if 0 <= step - 3 < UNITS:
+                            group(step - 3, 0)
+                        if live and tile_no + 1 < TILES:
+                            mask_part(tile_no + 1, hd)
+                    if live and q != 2:
+                        bend(step, max(q - 1, 0) if q == 3 else q, q + 1)
                     if q == 1 and 0 <= step - 1 < UNITS:
                         bend_max(step - 1)
                     if q == 2 and 0 <= step - 1 < UNITS:
                         shift_max(step - 1)
-                    if hd == 1 and step >= H + 1:
-                        gain_step(tile_no - 1, q - 1)
-                if 0 <= step - 2 < UNITS:
-                    group(step - 2, 1)
+                    if hd == 1 and step >= H + 1 and q < 3:
+                        gain_step(tile_no - 1, q)
+                if live and hd == 2 and tile_no + 1 < TILES:
+                    make_weight(tile_no + 1)
+                if 0 <= step - 4 < UNITS:
+                    quantise(step - 4)
+                if 0 <= step - 3 < UNITS:
+                    group(step - 3, 1)
                 if live:
                     row_max(step)
+                if hd == 0 and step >= 2 * H:
+                    finish(tile_no - 2)
                 if 0 <= step - 1 < UNITS:
                     exponential(step - 1)
-                    turn(step - 1)
-                if hd == 2 and step >= H + 2:
-                    finish(tile_no - 1)
+                if 0 <= step - 2 < UNITS:
+                    turn(step - 2)

@@ -250,6 +250,13 @@ def tile_gatlayersinglebatch_pa_kernel(tc, h, a, kernel, f_self, f_other, out):
             nc.scalar.activation(out=z[:, cols], in_=t[:, cols], func=ACT.Relu, scale=-(1.0 - SLOPE))
             nc.gpsimd.tensor_tensor(out=z[:, cols], in0=t[:, cols], in1=z[:, cols], op=ALU.add)
 
+        def bend_rest(i, first):
+            t = t_of[i]
+            rest = slice(first * BANK, N)
+            nc.vector.scalar_tensor_tensor(
+                out=z_of[i][:, rest], in0=t[:, rest], scalar=SLOPE, in1=t[:, rest], op0=ALU.mult, op1=ALU.max
+            )
+
         def row_max(i):
             top = small.tile([P, 1], F32, tag="top")
             nc.vector.tensor_reduce(out=top[:], in_=t_of[i][:], axis=AX.X, op=ALU.max)
@@ -303,10 +310,7 @@ def tile_gatlayersinglebatch_pa_kernel(tc, h, a, kernel, f_self, f_other, out):
             grp32 = grp_of[i][:].bitcast(F32).rearrange("p (g n u) -> p g n u", g=PASSES, u=2)
             dst = grp32[:, 2 * half : 2 * half + 2, :, :]
             src = tr_of[i, half][:].rearrange("p g u n -> p g n u")
-            if half == 0:
-                nc.scalar.copy(out=dst, in_=src)
-            else:
-                nc.vector.tensor_copy(out=dst, in_=src)
+            nc.scalar.copy(out=dst, in_=src)
 
         def quantise(i):
             codes = emp.tile([P, PASSES * P], U32, tag="codes", align_bytes=64)
@@ -380,20 +384,22 @@ def tile_gatlayersinglebatch_pa_kernel(tc, h, a, kernel, f_self, f_other, out):
                             group(step - 3, 0)
                         if live and tile_no + 1 < TILES:
                             mask_part(tile_no + 1, hd)
-                    if live and q != 2:
-                        bend(step, max(q - 1, 0) if q == 3 else q, q + 1)
+                    if live and q == CHUNKS - 2:
+                        bend(step, 0, CHUNKS - 1)
                     if q == 1 and 0 <= step - 1 < UNITS:
                         bend_max(step - 1)
                     if q == 2 and 0 <= step - 1 < UNITS:
                         shift_max(step - 1)
                     if hd == 1 and step >= H + 1 and q < 3:
                         gain_step(tile_no - 1, q)
+                if 0 <= step - 3 < UNITS:
+                    group(step - 3, 1)
+                if live:
+                    bend_rest(step, CHUNKS - 1)
                 if live and hd == 2 and tile_no + 1 < TILES:
                     make_weight(tile_no + 1)
                 if 0 <= step - 4 < UNITS:
                     quantise(step - 4)
-                if 0 <= step - 3 < UNITS:
-                    group(step - 3, 1)
                 if live:
                     row_max(step)
                 if hd == 0 and step >= 2 * H:

@@ -297,6 +297,15 @@ def tile_gatlayersinglebatch_pa_kernel(tc, h, a, kernel, f_self, f_other, out):
             words = em_of[i][:].bitcast(F32)
             for half in range(2):
                 tr = psum_tr.tile([P, 2, 2, P], F32, tag="tr")
+                nc.tensor.matmul_mx(
+                    out=tr[:].rearrange("p g u n -> p (g u n)"),
+                    lhsT=f_codes[:, half, 0, :].bitcast(FP8X4),
+                    lhsT_scale=f_scales[:, half, 0, :],
+                    rhs=f_codes[:, half, :, :].rearrange("p h o -> p (h o)").bitcast(FP8X4),
+                    rhs_scale=f_scales[:, half, :, :].rearrange("p h o -> p (h o)"),
+                    start=True,
+                    stop=True,
+                )
                 for gg in range(2):
                     for u in range(2):
                         first = (2 * (2 * half + gg) + u) * P
@@ -363,11 +372,12 @@ def tile_gatlayersinglebatch_pa_kernel(tc, h, a, kernel, f_self, f_other, out):
         make_weight(0)
         for blk in range(TILES // 4):
             mask_part(0, blk)
+        mask_part(1, 0)
         engines = {mybir.EngineType.PE, mybir.EngineType.DVE, mybir.EngineType.Activation, mybir.EngineType.Pool}
         with tc.manual_schedule(engines=engines):
             for q in range(CHUNKS):
                 dense(0, q)
-            for step in range(UNITS + 5):
+            for step in range(UNITS + 4):
                 tile_no, hd = divmod(step, H)
                 live = step < UNITS
                 if hd == 0 and tile_no + 2 < TILES:
@@ -378,12 +388,8 @@ def tile_gatlayersinglebatch_pa_kernel(tc, h, a, kernel, f_self, f_other, out):
                     if step + 1 < UNITS:
                         dense(step + 1, q)
                     if q == 0:
-                        if 0 <= step - 5:
-                            aggregate(step - 5)
                         if 0 <= step - 3 < UNITS:
                             group(step - 3, 0)
-                        if live and tile_no + 1 < TILES:
-                            mask_part(tile_no + 1, hd)
                     if live and q == CHUNKS - 2:
                         bend(step, 0, CHUNKS - 1)
                     if q == 1 and 0 <= step - 1 < UNITS:
@@ -402,9 +408,14 @@ def tile_gatlayersinglebatch_pa_kernel(tc, h, a, kernel, f_self, f_other, out):
                     quantise(step - 4)
                 if live:
                     row_max(step)
-                if hd == 0 and step >= 2 * H:
-                    finish(tile_no - 2)
-                if 0 <= step - 1 < UNITS:
-                    exponential(step - 1)
+                ahead = step + H + 1
+                if ahead < UNITS:
+                    mask_part(ahead // H, ahead % H)
+                if 0 <= step - 4 < UNITS:
+                    aggregate(step - 4)
                 if 0 <= step - 2 < UNITS:
                     turn(step - 2)
+                if hd == 3 and step >= 2 * H - 1:
+                    finish(tile_no - 1)
+                if 0 <= step - 1 < UNITS:
+                    exponential(step - 1)

@@ -32,7 +32,8 @@ SCALE = 1.0 / math.sqrt(D)
 NO_EDGE_LOG = 69.0
 EDGE_SLOPE = 2.0**112
 LEAST_WEIGHT = 2.0**-60
-FLOOR = -(2.0**30)
+LARGEST = 3.0e38
+CEILING = 2.0**30
 TINY = 1.0e-30
 
 FLOPS = 2 * N * F * H * O + 2 * H * N * N * D + 2 * H * N * N * O
@@ -171,8 +172,6 @@ def tile_gatlayersinglebatch_pa_kernel(tc, h, a, kernel, f_self, f_other, out):
         banks_of = {}
         t_of = {}
         z_of = {}
-        top_of = {}
-        bent_of = {}
         shift_of = {}
         em_of = {}
         tr_of = {}
@@ -187,12 +186,19 @@ def tile_gatlayersinglebatch_pa_kernel(tc, h, a, kernel, f_self, f_other, out):
             nc.sync.dma_start(out=adj_t[:], in_=adj_rows[tile_no // 2, tile_no % 2])
             adj_of[tile_no] = adj_t
 
-        def make_weight(tile_no):
-            weight = adjp.tile([P, N], BF16, tag="weight")
-            nc.vector.tensor_scalar(
-                out=weight[:], in0=adj_of[tile_no][:], scalar1=-1.0, scalar2=-LEAST_WEIGHT, op0=ALU.mult, op1=ALU.min
+        def weight_part(tile_no, q):
+            if q == 0:
+                weight = adjp.tile([P, N], BF16, tag="weight")
+                weight_of[tile_no] = weight
+            cols = slice(q * BANK, (q + 1) * BANK)
+            nc.gpsimd.tensor_scalar(
+                out=weight_of[tile_no][:, cols],
+                in0=adj_of[tile_no][:, cols],
+                scalar1=LARGEST,
+                scalar2=LEAST_WEIGHT,
+                op0=ALU.min,
+                op1=ALU.max,
             )
-            weight_of[tile_no] = weight
 
         def mask_part(tile_no, blk):
             if blk == 0:
@@ -240,40 +246,32 @@ def tile_gatlayersinglebatch_pa_kernel(tc, h, a, kernel, f_self, f_other, out):
                 out=t_of[i][:, cols], in0=banks_of[i, q][:], in1=weight_of[i // H][:, cols], op=ALU.mult
             )
 
-        def bend(i, first, last):
-            if first == 0:
-                z = zp.tile([P, N], F32, tag="z")
-                z_of[i] = z
-            cols = slice(first * BANK, last * BANK)
+        def bend(i, first):
+            z = zp.tile([P, N], F32, tag="z")
+            z_of[i] = z
+            cols = slice(first * BANK, N)
             t = t_of[i]
             z = z_of[i]
-            nc.scalar.activation(out=z[:, cols], in_=t[:, cols], func=ACT.Relu, scale=-(1.0 - SLOPE))
-            nc.gpsimd.tensor_tensor(out=z[:, cols], in0=t[:, cols], in1=z[:, cols], op=ALU.add)
+            nc.scalar.activation(out=z[:, cols], in_=t[:, cols], func=ACT.Relu, scale=1.0 - SLOPE)
+            nc.gpsimd.tensor_tensor(out=z[:, cols], in0=t[:, cols], in1=z[:, cols], op=ALU.subtract)
 
-        def bend_rest(i, first):
+        def bend_own(i, last):
             t = t_of[i]
-            rest = slice(first * BANK, N)
+            own = slice(0, last * BANK)
             nc.vector.scalar_tensor_tensor(
-                out=z_of[i][:, rest], in0=t[:, rest], scalar=SLOPE, in1=t[:, rest], op0=ALU.mult, op1=ALU.max
+                out=z_of[i][:, own], in0=t[:, own], scalar=SLOPE, in1=t[:, own], op0=ALU.mult, op1=ALU.min
             )
 
-        def row_max(i):
+        def row_min(i):
             top = small.tile([P, 1], F32, tag="top")
-            nc.vector.tensor_reduce(out=top[:], in_=t_of[i][:], axis=AX.X, op=ALU.max)
-            top_of[i] = top
-
-        def bend_max(i):
-            top = top_of[i]
+            nc.vector.tensor_reduce(out=top[:], in_=t_of[i][:], axis=AX.X, op=ALU.min)
             bent = small.tile([P, 1], F32, tag="bent")
-            nc.vector.tensor_scalar(
-                out=bent[:], in0=top[:], scalar1=SLOPE, scalar2=top[:, 0:1], op0=ALU.mult, op1=ALU.max
+            nc.gpsimd.tensor_scalar(
+                out=bent[:], in0=top[:], scalar1=SLOPE, scalar2=top[:, 0:1], op0=ALU.mult, op1=ALU.min
             )
-            bent_of[i] = bent
-
-        def shift_max(i):
             shift = small.tile([P, 1], F32, tag="shift")
-            nc.vector.tensor_scalar(
-                out=shift[:], in0=bent_of[i][:], scalar1=FLOOR, scalar2=-SCALE, op0=ALU.max, op1=ALU.mult
+            nc.gpsimd.tensor_scalar(
+                out=shift[:], in0=bent[:], scalar1=CEILING, scalar2=SCALE, op0=ALU.min, op1=ALU.mult
             )
             shift_of[i] = shift
 
@@ -288,7 +286,7 @@ def tile_gatlayersinglebatch_pa_kernel(tc, h, a, kernel, f_self, f_other, out):
                 in_=z_of[i][:],
                 func=ACT.Exp,
                 bias=shift_of[i][:, 0:1],
-                scale=SCALE,
+                scale=-SCALE,
                 accum_out=den_of[tile_no][:, hd : hd + 1],
             )
             em_of[i] = em
@@ -348,11 +346,11 @@ def tile_gatlayersinglebatch_pa_kernel(tc, h, a, kernel, f_self, f_other, out):
             if part == 0:
                 gain = small.tile([P, H], F32, tag="gain")
                 gain_of[tile_no] = gain
-                nc.vector.tensor_scalar_max(out=gain[:], in0=den_of[tile_no][:], scalar1=TINY)
+                nc.gpsimd.tensor_scalar_max(out=gain[:], in0=den_of[tile_no][:], scalar1=TINY)
             elif part == 1:
                 nc.vector.reciprocal(out=gain_of[tile_no][:], in_=gain_of[tile_no][:])
             else:
-                nc.vector.tensor_scalar_mul(
+                nc.gpsimd.tensor_scalar_mul(
                     out=gain_of[tile_no][:], in0=gain_of[tile_no][:], scalar1=rowmask[:, tile_no : tile_no + 1]
                 )
 
@@ -369,9 +367,11 @@ def tile_gatlayersinglebatch_pa_kernel(tc, h, a, kernel, f_self, f_other, out):
 
         load_adj(0)
         load_adj(1)
-        make_weight(0)
+        for q in range(CHUNKS):
+            weight_part(0, q)
         for blk in range(TILES // 4):
             mask_part(0, blk)
+        weight_part(1, 0)
         mask_part(1, 0)
         engines = {mybir.EngineType.PE, mybir.EngineType.DVE, mybir.EngineType.Activation, mybir.EngineType.Pool}
         with tc.manual_schedule(engines=engines):
@@ -387,29 +387,25 @@ def tile_gatlayersinglebatch_pa_kernel(tc, h, a, kernel, f_self, f_other, out):
                         weigh(step, q)
                     if step + 1 < UNITS:
                         dense(step + 1, q)
-                    if q == 0:
-                        if 0 <= step - 3 < UNITS:
-                            group(step - 3, 0)
-                    if live and q == CHUNKS - 2:
-                        bend(step, 0, CHUNKS - 1)
-                    if q == 1 and 0 <= step - 1 < UNITS:
-                        bend_max(step - 1)
-                    if q == 2 and 0 <= step - 1 < UNITS:
-                        shift_max(step - 1)
-                    if hd == 1 and step >= H + 1 and q < 3:
-                        gain_step(tile_no - 1, q)
-                if 0 <= step - 3 < UNITS:
-                    group(step - 3, 1)
+                    if q == 0 and 0 <= step - 3 < UNITS:
+                        group(step - 3, 0)
+                        group(step - 3, 1)
                 if live:
-                    bend_rest(step, CHUNKS - 1)
-                if live and hd == 2 and tile_no + 1 < TILES:
-                    make_weight(tile_no + 1)
+                    bend(step, 1)
+                if live:
+                    bend_own(step, 1)
                 if 0 <= step - 4 < UNITS:
                     quantise(step - 4)
                 if live:
-                    row_max(step)
+                    row_min(step)
+                if hd == 1 and step >= H + 1:
+                    gain_step(tile_no - 1, 0)
+                if hd == 2 and step >= H + 2:
+                    gain_step(tile_no - 1, 1)
+                    gain_step(tile_no - 1, 2)
                 ahead = step + H + 1
                 if ahead < UNITS:
+                    weight_part(ahead // H, ahead % H)
                     mask_part(ahead // H, ahead % H)
                 if 0 <= step - 4 < UNITS:
                     aggregate(step - 4)

@@ -32,8 +32,9 @@ SCALE = 1.0 / math.sqrt(D)
 NO_EDGE_LOG = 69.0
 EDGE_SLOPE = 2.0**112
 LEAST_WEIGHT = 2.0**-60
-LARGEST = 3.0e38
+OWN = 384
 CEILING = 2.0**30
+FEATS_START = 4
 TINY = 1.0e-30
 
 FLOPS = 2 * N * F * H * O + 2 * H * N * N * D + 2 * H * N * N * O
@@ -48,13 +49,14 @@ def tile_gatlayersinglebatch_pa_kernel(tc, h, a, kernel, f_self, f_other, out):
     with ExitStack() as ctx:
         const = ctx.enter_context(tc.tile_pool(name="const", bufs=1))
         setup = ctx.enter_context(tc.tile_pool(name="setup", bufs=1))
-        raw = ctx.enter_context(tc.tile_pool(name="raw", bufs=4))
-        junkp = ctx.enter_context(tc.tile_pool(name="junk", bufs=2))
+        raw = ctx.enter_context(tc.tile_pool(name="raw", bufs=2))
+        fsp = ctx.enter_context(tc.tile_pool(name="fs", bufs=2))
         adjp = ctx.enter_context(tc.tile_pool(name="adj", bufs=3))
         maskp = ctx.enter_context(tc.tile_pool(name="maskp", bufs=2))
         tp = ctx.enter_context(tc.tile_pool(name="t", bufs=2))
         zp = ctx.enter_context(tc.tile_pool(name="z", bufs=2))
         emp = ctx.enter_context(tc.tile_pool(name="em", bufs=3))
+        codep = ctx.enter_context(tc.tile_pool(name="codes", bufs=8))
         small = ctx.enter_context(tc.tile_pool(name="small", bufs=3))
         outp = ctx.enter_context(tc.tile_pool(name="outp", bufs=2))
         psum_dense = ctx.enter_context(tc.psum_pool(name="psum_dense", bufs=4))
@@ -66,69 +68,83 @@ def tile_gatlayersinglebatch_pa_kernel(tc, h, a, kernel, f_self, f_other, out):
         masks.make_identity(nc, ident_bf[:])
         ident_f32 = const.tile([P, P], F32)
         masks.make_identity(nc, ident_f32[:])
+        log_bias = const.tile([P, 1], F32)
+        nc.vector.memset(log_bias[:], NO_EDGE_LOG)
+        ones = const.tile([P, 1], BF16)
+        nc.vector.memset(ones[:], 1.0)
 
-        fsT = const.tile([P, H, N], BF16)
         foT = const.tile([P, H, N], BF16)
-        for hd in range(H):
-            fo_raw = raw.tile([P, TILES, D], BF16, tag="fraw")
+        fo_raw_of = {}
+
+        def load_fo(hd):
+            fo_raw = raw.tile([P, TILES, D], BF16, tag="fo_raw")
             nc.sync.dma_start(out=fo_raw[:], in_=f_other[hd, :, :].rearrange("(t p) d -> p t d", p=P))
-            fs_raw = raw.tile([P, TILES, D], BF16, tag="fraw")
-            nc.sync.dma_start(
-                out=fs_raw[:].rearrange("p (c e) d -> p c e d", e=2),
-                in_=f_self[hd, :, :].rearrange("(c p e) d -> p c e d", p=P, e=2),
-            )
-            for src, dst in ((fo_raw, foT), (fs_raw, fsT)):
-                for blk in range(TILES // 4):
-                    pt = psum_dense.tile([P, 4, P], BF16, tag="dense")
-                    for k in range(4):
-                        nc.tensor.transpose(pt[:, k, :], src[:, 4 * blk + k, :], ident_bf[:])
-                    dst_cols = dst[:, hd, 4 * blk * P : 4 * (blk + 1) * P]
-                    if dst is fsT:
-                        nc.vector.tensor_scalar_mul(out=dst_cols, in0=pt[:].rearrange("p k n -> p (k n)"), scalar1=-1.0)
-                    else:
-                        nc.scalar.copy(out=dst_cols, in_=pt[:].rearrange("p k n -> p (k n)"))
+            fo_raw_of[hd] = fo_raw
+
+        def turn_fo(hd, blk, copy):
+            pt = psum_tr.tile([P, 4, P], BF16, tag="tr")
+            for k in range(4):
+                nc.tensor.transpose(pt[:, k, :], fo_raw_of[hd][:, 4 * blk + k, :], ident_bf[:])
+            copy(out=foT[:, hd, blk * BANK : (blk + 1) * BANK], in_=pt[:].rearrange("p k n -> p (k n)"))
+
+        fs_raw_of = {}
+        fsT_of = {}
+
+        def load_fs(pair):
+            fs_raw = fsp.tile([P, H, 2, D], BF16, tag="fs_raw")
+            nodes = slice(2 * pair * P, 2 * (pair + 1) * P)
+            nc.sync.dma_start(out=fs_raw[:], in_=f_self[:, nodes, :].rearrange("h (p e) d -> p h e d", e=2))
+            fs_raw_of[pair] = fs_raw
+
+        def turn_fs(tile_no):
+            pt = psum_mask.tile([P, H, P], BF16, tag="zt")
+            for hd in range(H):
+                nc.tensor.transpose(pt[:, hd, :], fs_raw_of[tile_no // 2][:, hd, tile_no % 2, :], ident_bf[:])
+            fsT = fsp.tile([P, H, P], BF16, tag="fsT")
+            nc.vector.tensor_scalar_mul(out=fsT[:], in0=pt[:], scalar1=-1.0)
+            fsT_of[tile_no] = fsT
 
         k_raw = setup.tile([P, H, PACK, O], BF16)
-        for hd in range(H):
-            nc.sync.dma_start(
-                out=k_raw[:, hd, :, :].rearrange("p (u e) o -> p u e o", u=2),
-                in_=kernel[hd, :, :].rearrange("(u p e) o -> p u e o", u=2, e=2),
-            )
         k_grp = setup.tile([P, H, O, PACK], BF16, align_bytes=64)
-        nc.vector.tensor_copy(out=k_grp[:], in_=k_raw[:].rearrange("p h t o -> p h o t"))
         k_codes = setup.tile([P, H * O], U32, align_bytes=64)
         k_scales = setup.tile([P, H * O], U8, align_bytes=64)
 
-        x_raw = setup.tile([P, TILES // 2, 2, F], BF16)
-        nc.sync.dma_start(out=x_raw[:], in_=x_rows)
-        x_grp = setup.tile([P, TILES * P * PACK], BF16, tag="grouped", align_bytes=64)
+        def load_kernel():
+            for hd in range(H):
+                nc.sync.dma_start(
+                    out=k_raw[:, hd, :, :].rearrange("p (u e) o -> p u e o", u=2),
+                    in_=kernel[hd, :, :].rearrange("(u p e) o -> p u e o", u=2, e=2),
+                )
+
+        def quantise_kernel():
+            nc.vector.quantize_mx(
+                out=k_codes[:].bitcast(FP8X4), scales=k_scales[:], in_=k_grp[:].rearrange("p h o t -> p (h o t)")
+            )
+
+        x_raw = setup.tile([P, TILES // 2, 2, F], BF16, tag="x_raw", align_bytes=64)
+        x_grp = setup.tile([P, TILES * P * PACK], BF16, align_bytes=64)
         x_grp32 = x_grp[:].bitcast(F32).rearrange("p (t n u) -> p t n u", t=TILES, u=2)
-        absum = const.tile([P, TILES], F32)
-        for pair in range(TILES // 2):
+        x_codes = setup.tile([P, TILES * P], U32, align_bytes=64)
+        x_scales = setup.tile([P, TILES * P], U8, align_bytes=64)
+        zero_of = {}
+        count_of = []
+        rowmask = const.tile([P, TILES], F32)
+
+        def load_x(part):
+            pairs = slice(2 * part, 2 * part + 2)
+            nc.sync.dma_start(out=x_raw[:, pairs, :, :], in_=x_rows[:, pairs, :, :])
+
+        def turn_x(pair):
             xt = psum_tr.tile([P, 2, 2, P], F32, tag="tr")
             for e in range(2):
                 words = x_raw[:, pair, e, :].bitcast(F32)
                 for u in range(2):
                     nc.tensor.transpose(xt[:, e, u, :], words[:, u * P : (u + 1) * P], ident_f32[:])
-                junk = junkp.tile([P, F], BF16)
-                nc.scalar.activation(
-                    out=junk[:],
-                    in_=x_raw[:, pair, e, :],
-                    func=ACT.Abs,
-                    accum_out=absum[:, 2 * pair + e : 2 * pair + e + 1],
-                )
             nc.vector.tensor_copy(
                 out=x_grp32[:, 2 * pair : 2 * pair + 2, :, :], in_=xt[:].rearrange("p t u n -> p t n u")
             )
-        rowmask = const.tile([P, TILES], F32)
-        nc.vector.tensor_single_scalar(out=rowmask[:], in_=absum[:], scalar=0.0, op=ALU.is_gt)
 
-        nc.vector.quantize_mx(
-            out=k_codes[:].bitcast(FP8X4), scales=k_scales[:], in_=k_grp[:].rearrange("p h o t -> p (h o t)")
-        )
-        x_codes = setup.tile([P, TILES * P], U32, align_bytes=64)
-        x_scales = setup.tile([P, TILES * P], U8, align_bytes=64)
-        for half in range(2):
+        def quantise_x(half):
             words = slice(half * 1024, (half + 1) * 1024)
             nc.vector.quantize_mx(
                 out=x_codes[:, words].bitcast(FP8X4),
@@ -136,35 +152,62 @@ def tile_gatlayersinglebatch_pa_kernel(tc, h, a, kernel, f_self, f_other, out):
                 in_=x_grp[:, half * 4096 : (half + 1) * 4096],
             )
 
-        f_grp = setup.tile([P, PASSES, H, O, PACK], BF16, tag="grouped", align_bytes=64)
+        def find_zeros(g):
+            zero = raw.tile([P, PACK, P, PACK], BF16, tag="zero")
+            nc.vector.tensor_single_scalar(
+                out=zero[:].rearrange("p t n k -> p (t n k)"),
+                in_=x_grp[:, g * N : (g + 1) * N],
+                scalar=0.0,
+                op=ALU.is_equal,
+            )
+            zero_of[g] = zero
+
+        def count_zeros(g):
+            if g == 0:
+                count = psum_acc.tile([P, TILES], F32, tag="acc")
+                count_of.append(count)
+            for t in range(PACK):
+                tile_no = PACK * g + t
+                for k in range(PACK):
+                    nc.tensor.matmul(
+                        count_of[0][:, tile_no : tile_no + 1],
+                        lhsT=zero_of[g][:, t, :, k],
+                        rhs=ones[:],
+                        start=(k == 0),
+                        stop=(k == PACK - 1),
+                    )
+
+        def mark_padding():
+            nc.vector.tensor_single_scalar(out=rowmask[:], in_=count_of[0][:], scalar=float(F), op=ALU.is_lt)
+
+        f_grp_of = []
         f_codes = const.tile([P, PASSES, H, O], U32, align_bytes=64)
         f_scales = const.tile([P, PASSES, H, O], U8, align_bytes=64)
-        for g in range(PASSES):
-            for hd in range(H):
-                fb = psum_dense.tile([P, PACK, O], F32, tag="dense")
-                for t in range(PACK):
-                    nodes = slice((PACK * g + t) * P, (PACK * g + t + 1) * P)
-                    nc.tensor.matmul_mx(
-                        out=fb[:, t, :],
-                        lhsT=x_codes[:, nodes].bitcast(FP8X4),
-                        lhsT_scale=x_scales[:, nodes],
-                        rhs=k_codes[:, hd * O : (hd + 1) * O].bitcast(FP8X4),
-                        rhs_scale=k_scales[:, hd * O : (hd + 1) * O],
-                        start=True,
-                        stop=True,
-                    )
-                if hd % 2 == 0:
-                    nc.vector.tensor_copy(out=f_grp[:, g, hd, :, :], in_=fb[:].rearrange("p t o -> p o t"))
-                else:
-                    nc.scalar.copy(out=f_grp[:, g, hd, :, :], in_=fb[:].rearrange("p t o -> p o t"))
+
+        def make_feats(g, hd):
+            if g == 0 and hd == 0:
+                f_grp = setup.tile([P, PASSES, H, O, PACK], BF16, tag="x_raw", align_bytes=64)
+                f_grp_of.append(f_grp)
+            fb = psum_tr.tile([P, PACK, O], F32, tag="tr")
+            for t in range(PACK):
+                nodes = slice((PACK * g + t) * P, (PACK * g + t + 1) * P)
+                nc.tensor.matmul_mx(
+                    out=fb[:, t, :],
+                    lhsT=x_codes[:, nodes].bitcast(FP8X4),
+                    lhsT_scale=x_scales[:, nodes],
+                    rhs=k_codes[:, hd * O : (hd + 1) * O].bitcast(FP8X4),
+                    rhs_scale=k_scales[:, hd * O : (hd + 1) * O],
+                    start=True,
+                    stop=True,
+                )
+            nc.scalar.copy(out=f_grp_of[0][:, g, hd, :, :], in_=fb[:].rearrange("p t o -> p o t"))
+
+        def quantise_feats(g):
             nc.vector.quantize_mx(
                 out=f_codes[:, g, :, :].rearrange("p h o -> p (h o)").bitcast(FP8X4),
                 scales=f_scales[:, g, :, :].rearrange("p h o -> p (h o)"),
-                in_=f_grp[:, g, :, :, :].rearrange("p h o t -> p (h o t)"),
+                in_=f_grp_of[0][:, g, :, :, :].rearrange("p h o t -> p (h o t)"),
             )
-
-        log_bias = const.tile([P, 1], F32)
-        nc.vector.memset(log_bias[:], NO_EDGE_LOG)
 
         adj_of = {}
         mask_of = {}
@@ -172,6 +215,8 @@ def tile_gatlayersinglebatch_pa_kernel(tc, h, a, kernel, f_self, f_other, out):
         banks_of = {}
         t_of = {}
         z_of = {}
+        top_of = {}
+        bent_of = {}
         shift_of = {}
         em_of = {}
         tr_of = {}
@@ -186,26 +231,17 @@ def tile_gatlayersinglebatch_pa_kernel(tc, h, a, kernel, f_self, f_other, out):
             nc.sync.dma_start(out=adj_t[:], in_=adj_rows[tile_no // 2, tile_no % 2])
             adj_of[tile_no] = adj_t
 
-        def weight_part(tile_no, q):
-            if q == 0:
-                weight = adjp.tile([P, N], BF16, tag="weight")
-                weight_of[tile_no] = weight
-            cols = slice(q * BANK, (q + 1) * BANK)
-            nc.gpsimd.tensor_scalar(
-                out=weight_of[tile_no][:, cols],
-                in0=adj_of[tile_no][:, cols],
-                scalar1=LARGEST,
-                scalar2=LEAST_WEIGHT,
-                op0=ALU.min,
-                op1=ALU.max,
-            )
+        def make_weight(tile_no):
+            weight = maskp.tile([P, N], BF16, tag="weight")
+            nc.vector.tensor_scalar_max(out=weight[:], in0=adj_of[tile_no][:], scalar1=LEAST_WEIGHT)
+            weight_of[tile_no] = weight
 
-        def mask_part(tile_no, blk):
+        def mask_part(psum, tag, tile_no, blk):
             if blk == 0:
                 maskT = maskp.tile([P, TILES, P], F32, tag="maskT")
                 mask_of[tile_no] = maskT
             adj_t = adj_of[tile_no]
-            zt = psum_mask.tile([P, 4, P], BF16, tag="zt")
+            zt = psum.tile([P, 4, P], BF16, tag=tag)
             for k in range(4):
                 nc.tensor.transpose(zt[:, k, :], adj_t[:, (4 * blk + k) * P : (4 * blk + k + 1) * P], ident_bf[:])
             nc.scalar.activation(
@@ -221,7 +257,7 @@ def tile_gatlayersinglebatch_pa_kernel(tc, h, a, kernel, f_self, f_other, out):
             bank = psum_dense.tile([P, BANK], F32, tag="dense")
             nc.tensor.matmul(
                 bank[:],
-                lhsT=fsT[:, hd, tile_no * P : (tile_no + 1) * P],
+                lhsT=fsT_of[tile_no][:, hd, :],
                 rhs=foT[:, hd, q * BANK : (q + 1) * BANK],
                 start=True,
                 stop=False,
@@ -246,18 +282,18 @@ def tile_gatlayersinglebatch_pa_kernel(tc, h, a, kernel, f_self, f_other, out):
                 out=t_of[i][:, cols], in0=banks_of[i, q][:], in1=weight_of[i // H][:, cols], op=ALU.mult
             )
 
-        def bend(i, first):
+        def bend(i):
             z = zp.tile([P, N], F32, tag="z")
             z_of[i] = z
-            cols = slice(first * BANK, N)
+            cols = slice(OWN, N)
             t = t_of[i]
             z = z_of[i]
             nc.scalar.activation(out=z[:, cols], in_=t[:, cols], func=ACT.Relu, scale=1.0 - SLOPE)
             nc.gpsimd.tensor_tensor(out=z[:, cols], in0=t[:, cols], in1=z[:, cols], op=ALU.subtract)
 
-        def bend_own(i, last):
+        def bend_own(i):
             t = t_of[i]
-            own = slice(0, last * BANK)
+            own = slice(0, OWN)
             nc.vector.scalar_tensor_tensor(
                 out=z_of[i][:, own], in0=t[:, own], scalar=SLOPE, in1=t[:, own], op0=ALU.mult, op1=ALU.min
             )
@@ -265,13 +301,20 @@ def tile_gatlayersinglebatch_pa_kernel(tc, h, a, kernel, f_self, f_other, out):
         def row_min(i):
             top = small.tile([P, 1], F32, tag="top")
             nc.vector.tensor_reduce(out=top[:], in_=t_of[i][:], axis=AX.X, op=ALU.min)
+            top_of[i] = top
+
+        def bend_min(i):
+            top = top_of[i]
             bent = small.tile([P, 1], F32, tag="bent")
-            nc.gpsimd.tensor_scalar(
+            nc.vector.tensor_scalar(
                 out=bent[:], in0=top[:], scalar1=SLOPE, scalar2=top[:, 0:1], op0=ALU.mult, op1=ALU.min
             )
+            bent_of[i] = bent
+
+        def shift_min(i):
             shift = small.tile([P, 1], F32, tag="shift")
-            nc.gpsimd.tensor_scalar(
-                out=shift[:], in0=bent[:], scalar1=CEILING, scalar2=SCALE, op0=ALU.min, op1=ALU.mult
+            nc.vector.tensor_scalar(
+                out=shift[:], in0=bent_of[i][:], scalar1=CEILING, scalar2=SCALE, op0=ALU.min, op1=ALU.mult
             )
             shift_of[i] = shift
 
@@ -291,19 +334,28 @@ def tile_gatlayersinglebatch_pa_kernel(tc, h, a, kernel, f_self, f_other, out):
             )
             em_of[i] = em
 
-        def turn(i):
+        def warm(bank, g):
+            nc.tensor.matmul_mx(
+                out=bank,
+                lhsT=f_codes[:, g, 0, :].bitcast(FP8X4),
+                lhsT_scale=f_scales[:, g, 0, :],
+                rhs=f_codes[:, g, :, :].rearrange("p h o -> p (h o)").bitcast(FP8X4),
+                rhs_scale=f_scales[:, g, :, :].rearrange("p h o -> p (h o)"),
+                start=True,
+                stop=True,
+            )
+
+        def warm_twice():
+            idle = psum_mask.tile([P, BANK], F32, tag="zt")
+            warm(idle[:], 0)
+            warm(idle[:], 1)
+
+        def turn(i, keep_warm):
             words = em_of[i][:].bitcast(F32)
             for half in range(2):
                 tr = psum_tr.tile([P, 2, 2, P], F32, tag="tr")
-                nc.tensor.matmul_mx(
-                    out=tr[:].rearrange("p g u n -> p (g u n)"),
-                    lhsT=f_codes[:, half, 0, :].bitcast(FP8X4),
-                    lhsT_scale=f_scales[:, half, 0, :],
-                    rhs=f_codes[:, half, :, :].rearrange("p h o -> p (h o)").bitcast(FP8X4),
-                    rhs_scale=f_scales[:, half, :, :].rearrange("p h o -> p (h o)"),
-                    start=True,
-                    stop=True,
-                )
+                if keep_warm and half == 0:
+                    warm(tr[:].rearrange("p g u n -> p (g u n)"), half)
                 for gg in range(2):
                     for u in range(2):
                         first = (2 * (2 * half + gg) + u) * P
@@ -320,8 +372,8 @@ def tile_gatlayersinglebatch_pa_kernel(tc, h, a, kernel, f_self, f_other, out):
             nc.scalar.copy(out=dst, in_=src)
 
         def quantise(i):
-            codes = emp.tile([P, PASSES * P], U32, tag="codes", align_bytes=64)
-            scales = emp.tile([P, PASSES * P], U8, tag="scales", align_bytes=64)
+            codes = codep.tile([P, PASSES * P], U32, tag="codes", align_bytes=64)
+            scales = codep.tile([P, PASSES * P], U8, tag="scales", align_bytes=64)
             nc.vector.quantize_mx(out=codes[:].bitcast(FP8X4), scales=scales[:], in_=grp_of[i][:])
             codes_of[i] = (codes, scales)
 
@@ -346,11 +398,11 @@ def tile_gatlayersinglebatch_pa_kernel(tc, h, a, kernel, f_self, f_other, out):
             if part == 0:
                 gain = small.tile([P, H], F32, tag="gain")
                 gain_of[tile_no] = gain
-                nc.gpsimd.tensor_scalar_max(out=gain[:], in0=den_of[tile_no][:], scalar1=TINY)
+                nc.vector.tensor_scalar_max(out=gain[:], in0=den_of[tile_no][:], scalar1=TINY)
             elif part == 1:
                 nc.vector.reciprocal(out=gain_of[tile_no][:], in_=gain_of[tile_no][:])
             else:
-                nc.gpsimd.tensor_scalar_mul(
+                nc.vector.tensor_scalar_mul(
                     out=gain_of[tile_no][:], in0=gain_of[tile_no][:], scalar1=rowmask[:, tile_no : tile_no + 1]
                 )
 
@@ -366,52 +418,100 @@ def tile_gatlayersinglebatch_pa_kernel(tc, h, a, kernel, f_self, f_other, out):
             nc.sync.dma_start(out=out_rows[tile_no // 2, tile_no % 2], in_=o_sb[:].rearrange("p h o -> p (h o)"))
 
         load_adj(0)
+        load_fo(0)
+        load_fs(0)
+        load_fo(1)
         load_adj(1)
-        for q in range(CHUNKS):
-            weight_part(0, q)
-        for blk in range(TILES // 4):
-            mask_part(0, blk)
-        weight_part(1, 0)
-        mask_part(1, 0)
+        load_kernel()
+        load_fo(2)
+        load_fo(3)
+        for part in range(TILES // 4):
+            load_x(part)
         engines = {mybir.EngineType.PE, mybir.EngineType.DVE, mybir.EngineType.Activation, mybir.EngineType.Pool}
         with tc.manual_schedule(engines=engines):
+            for blk in range(TILES // 4):
+                mask_part(psum_dense, "dense", 0, blk)
+            make_weight(0)
+            turn_fs(0)
+            for blk in range(TILES // 4):
+                turn_fo(0, blk, nc.vector.tensor_copy)
             for q in range(CHUNKS):
                 dense(0, q)
+            waiting = []
+            finished = 0
             for step in range(UNITS + 4):
                 tile_no, hd = divmod(step, H)
                 live = step < UNITS
                 if hd == 0 and tile_no + 2 < TILES:
                     load_adj(tile_no + 2)
+                    if tile_no % 2 == 0:
+                        load_fs(tile_no // 2 + 1)
+                if step + 1 < H:
+                    for blk in range(TILES // 4):
+                        turn_fo(step + 1, blk, nc.scalar.copy)
+                if step == 7:
+                    mark_padding()
                 for q in range(CHUNKS):
                     if live:
                         weigh(step, q)
                     if step + 1 < UNITS:
                         dense(step + 1, q)
+                    if q == 1 and 0 <= step - 1 < UNITS:
+                        bend_min(step - 1)
+                    if q == 2 and 0 <= step - 1 < UNITS:
+                        shift_min(step - 1)
+                    if hd == 3 and step >= 2 * H - 1 and q < 3:
+                        gain_step(tile_no - 1, q)
                     if q == 0 and 0 <= step - 3 < UNITS:
                         group(step - 3, 0)
                         group(step - 3, 1)
+                    if q == 1 and 0 <= step - FEATS_START < PASSES:
+                        make_feats(step - FEATS_START, 0)
+                        make_feats(step - FEATS_START, 1)
                 if live:
-                    bend(step, 1)
+                    bend(step)
                 if live:
-                    bend_own(step, 1)
+                    bend_own(step)
+                if live and hd == 2 and tile_no + 1 < TILES:
+                    make_weight(tile_no + 1)
                 if 0 <= step - 4 < UNITS:
                     quantise(step - 4)
+                    waiting.append(step - 4)
+                if step == 0:
+                    nc.vector.tensor_copy(out=k_grp[:], in_=k_raw[:].rearrange("p h t o -> p h o t"))
+                if step in (1, 2):
+                    for pair in range(4):
+                        turn_x(4 * (step - 1) + pair)
+                if step in (3, 4):
+                    quantise_x(step - 3)
+                if 0 <= step - 3 < PASSES:
+                    find_zeros(step - 3)
+                    count_zeros(step - 3)
+                if 0 <= step - FEATS_START - 1 < PASSES:
+                    quantise_feats(step - FEATS_START - 1)
                 if live:
                     row_min(step)
-                if hd == 1 and step >= H + 1:
-                    gain_step(tile_no - 1, 0)
-                if hd == 2 and step >= H + 2:
-                    gain_step(tile_no - 1, 1)
-                    gain_step(tile_no - 1, 2)
-                ahead = step + H + 1
-                if ahead < UNITS:
-                    weight_part(ahead // H, ahead % H)
-                    mask_part(ahead // H, ahead % H)
-                if 0 <= step - 4 < UNITS:
-                    aggregate(step - 4)
+                if step == 0:
+                    quantise_kernel()
+                if 0 <= step - FEATS_START < PASSES:
+                    make_feats(step - FEATS_START, 2)
+                    make_feats(step - FEATS_START, 3)
+                for ahead in range(step + H if step == 0 else step + H + 1, step + H + 2):
+                    if ahead < UNITS:
+                        mask_part(psum_mask, "zt", ahead // H, ahead % H)
+                        if ahead % H == 2:
+                            turn_fs(ahead // H)
+                ready = step > FEATS_START + PASSES
+                units = [unit for unit in waiting[:2] if ready and unit // H == finished]
+                waiting = waiting[len(units) :]
+                for unit in units:
+                    aggregate(unit)
                 if 0 <= step - 2 < UNITS:
-                    turn(step - 2)
-                if hd == 3 and step >= 2 * H - 1:
-                    finish(tile_no - 1)
+                    turn(step - 2, ready)
+                if ready and live:
+                    warm_twice()
+                if units and units[-1] % H == H - 1:
+                    finish(finished)
+                    finished += 1
                 if 0 <= step - 1 < UNITS:
                     exponential(step - 1)

@@ -334,28 +334,10 @@ def tile_gatlayersinglebatch_pa_kernel(tc, h, a, kernel, f_self, f_other, out):
             )
             em_of[i] = em
 
-        def warm(bank, g):
-            nc.tensor.matmul_mx(
-                out=bank,
-                lhsT=f_codes[:, g, 0, :].bitcast(FP8X4),
-                lhsT_scale=f_scales[:, g, 0, :],
-                rhs=f_codes[:, g, :, :].rearrange("p h o -> p (h o)").bitcast(FP8X4),
-                rhs_scale=f_scales[:, g, :, :].rearrange("p h o -> p (h o)"),
-                start=True,
-                stop=True,
-            )
-
-        def warm_twice():
-            idle = psum_mask.tile([P, BANK], F32, tag="zt")
-            warm(idle[:], 0)
-            warm(idle[:], 1)
-
-        def turn(i, keep_warm):
+        def turn(i):
             words = em_of[i][:].bitcast(F32)
             for half in range(2):
                 tr = psum_tr.tile([P, 2, 2, P], F32, tag="tr")
-                if keep_warm and half == 0:
-                    warm(tr[:].rearrange("p g u n -> p (g u n)"), half)
                 for gg in range(2):
                     for u in range(2):
                         first = (2 * (2 * half + gg) + u) * P
@@ -507,9 +489,7 @@ def tile_gatlayersinglebatch_pa_kernel(tc, h, a, kernel, f_self, f_other, out):
                 for unit in units:
                     aggregate(unit)
                 if 0 <= step - 2 < UNITS:
-                    turn(step - 2, ready)
-                if ready and live:
-                    warm_twice()
+                    turn(step - 2)
                 if units and units[-1] % H == H - 1:
                     finish(finished)
                     finished += 1

@@ -32,7 +32,7 @@ SCALE = 1.0 / math.sqrt(D)
 NO_EDGE_LOG = 69.0
 EDGE_SLOPE = 2.0**112
 LEAST_WEIGHT = 2.0**-60
-OWN = 384
+OWN = 512
 CEILING = 2.0**30
 FEATS_START = 4
 TINY = 1.0e-30
@@ -49,7 +49,8 @@ def tile_gatlayersinglebatch_pa_kernel(tc, h, a, kernel, f_self, f_other, out):
     with ExitStack() as ctx:
         const = ctx.enter_context(tc.tile_pool(name="const", bufs=1))
         setup = ctx.enter_context(tc.tile_pool(name="setup", bufs=1))
-        raw = ctx.enter_context(tc.tile_pool(name="raw", bufs=2))
+        raw = ctx.enter_context(tc.tile_pool(name="raw", bufs=4))
+        zerop = ctx.enter_context(tc.tile_pool(name="zerop", bufs=2))
         fsp = ctx.enter_context(tc.tile_pool(name="fs", bufs=2))
         adjp = ctx.enter_context(tc.tile_pool(name="adj", bufs=3))
         maskp = ctx.enter_context(tc.tile_pool(name="maskp", bufs=2))
@@ -88,6 +89,7 @@ def tile_gatlayersinglebatch_pa_kernel(tc, h, a, kernel, f_self, f_other, out):
             copy(out=foT[:, hd, blk * BANK : (blk + 1) * BANK], in_=pt[:].rearrange("p k n -> p (k n)"))
 
         fs_raw_of = {}
+        fs_turned_of = {}
         fsT_of = {}
 
         def load_fs(pair):
@@ -100,8 +102,11 @@ def tile_gatlayersinglebatch_pa_kernel(tc, h, a, kernel, f_self, f_other, out):
             pt = psum_mask.tile([P, H, P], BF16, tag="zt")
             for hd in range(H):
                 nc.tensor.transpose(pt[:, hd, :], fs_raw_of[tile_no // 2][:, hd, tile_no % 2, :], ident_bf[:])
+            fs_turned_of[tile_no] = pt
+
+        def negate_fs(tile_no):
             fsT = fsp.tile([P, H, P], BF16, tag="fsT")
-            nc.vector.tensor_scalar_mul(out=fsT[:], in0=pt[:], scalar1=-1.0)
+            nc.vector.tensor_scalar_mul(out=fsT[:], in0=fs_turned_of[tile_no][:], scalar1=-1.0)
             fsT_of[tile_no] = fsT
 
         k_raw = setup.tile([P, H, PACK, O], BF16)
@@ -153,7 +158,7 @@ def tile_gatlayersinglebatch_pa_kernel(tc, h, a, kernel, f_self, f_other, out):
             )
 
         def find_zeros(g):
-            zero = raw.tile([P, PACK, P, PACK], BF16, tag="zero")
+            zero = zerop.tile([P, PACK, P, PACK], BF16, tag="zero")
             nc.vector.tensor_single_scalar(
                 out=zero[:].rearrange("p t n k -> p (t n k)"),
                 in_=x_grp[:, g * N : (g + 1) * N],
@@ -210,6 +215,7 @@ def tile_gatlayersinglebatch_pa_kernel(tc, h, a, kernel, f_self, f_other, out):
             )
 
         adj_of = {}
+        zt_of = {}
         mask_of = {}
         weight_of = {}
         banks_of = {}
@@ -236,42 +242,47 @@ def tile_gatlayersinglebatch_pa_kernel(tc, h, a, kernel, f_self, f_other, out):
             nc.vector.tensor_scalar_max(out=weight[:], in0=adj_of[tile_no][:], scalar1=LEAST_WEIGHT)
             weight_of[tile_no] = weight
 
-        def mask_part(psum, tag, tile_no, blk):
-            if blk == 0:
-                maskT = maskp.tile([P, TILES, P], F32, tag="maskT")
-                mask_of[tile_no] = maskT
+        def turn_adj(psum, tag, tile_no, blk):
             adj_t = adj_of[tile_no]
             zt = psum.tile([P, 4, P], BF16, tag=tag)
             for k in range(4):
                 nc.tensor.transpose(zt[:, k, :], adj_t[:, (4 * blk + k) * P : (4 * blk + k + 1) * P], ident_bf[:])
+            zt_of[tile_no, blk] = zt
+
+        def make_mask(tile_no, blk):
+            if blk == 0:
+                maskT = maskp.tile([P, TILES, P], F32, tag="maskT")
+                mask_of[tile_no] = maskT
             nc.scalar.activation(
                 out=mask_of[tile_no][:, 4 * blk : 4 * blk + 4, :],
-                in_=zt[:],
+                in_=zt_of[tile_no, blk][:],
                 func=ACT.Exp,
                 bias=log_bias[:, 0:1],
                 scale=-EDGE_SLOPE,
             )
 
-        def dense(i, q):
+        def dense(i, first):
             tile_no, hd = divmod(i, H)
-            bank = psum_dense.tile([P, BANK], F32, tag="dense")
-            nc.tensor.matmul(
-                bank[:],
-                lhsT=fsT_of[tile_no][:, hd, :],
-                rhs=foT[:, hd, q * BANK : (q + 1) * BANK],
-                start=True,
-                stop=False,
-            )
-            for k in range(4):
+            for q in (first, first + 1):
+                bank = psum_dense.tile([P, BANK], F32, tag="dense")
                 nc.tensor.matmul(
-                    bank[:, k * P : (k + 1) * P],
-                    lhsT=mask_of[tile_no][:, 4 * q + k, :],
-                    rhs=ident_f32[:],
-                    is_transpose=True,
-                    start=False,
-                    stop=(k == 3),
+                    bank[:],
+                    lhsT=fsT_of[tile_no][:, hd, :],
+                    rhs=foT[:, hd, q * BANK : (q + 1) * BANK],
+                    start=True,
+                    stop=False,
                 )
-            banks_of[i, q] = bank
+                banks_of[i, q] = bank
+            for q in (first, first + 1):
+                for k in range(4):
+                    nc.tensor.matmul(
+                        banks_of[i, q][:, k * P : (k + 1) * P],
+                        lhsT=mask_of[tile_no][:, 4 * q + k, :],
+                        rhs=ident_f32[:],
+                        is_transpose=True,
+                        start=False,
+                        stop=(k == 3),
+                    )
 
         def weigh(i, q):
             if q == 0:
@@ -282,14 +293,16 @@ def tile_gatlayersinglebatch_pa_kernel(tc, h, a, kernel, f_self, f_other, out):
                 out=t_of[i][:, cols], in0=banks_of[i, q][:], in1=weight_of[i // H][:, cols], op=ALU.mult
             )
 
-        def bend(i):
-            z = zp.tile([P, N], F32, tag="z")
-            z_of[i] = z
-            cols = slice(OWN, N)
+        def bend(i, first, last):
             t = t_of[i]
-            z = z_of[i]
-            nc.scalar.activation(out=z[:, cols], in_=t[:, cols], func=ACT.Relu, scale=1.0 - SLOPE)
-            nc.gpsimd.tensor_tensor(out=z[:, cols], in0=t[:, cols], in1=z[:, cols], op=ALU.subtract)
+            if first == OWN:
+                z = zp.tile([P, N], F32, tag="z")
+                z_of[i] = z
+            cols = slice(first, last)
+            nc.scalar.activation(out=z_of[i][:, cols], in_=t[:, cols], func=ACT.Relu, scale=1.0 - SLOPE)
+            if last == N:
+                cols = slice(OWN, N)
+                nc.gpsimd.tensor_tensor(out=z_of[i][:, cols], in0=t[:, cols], in1=z_of[i][:, cols], op=ALU.subtract)
 
         def bend_own(i):
             t = t_of[i]
@@ -412,46 +425,69 @@ def tile_gatlayersinglebatch_pa_kernel(tc, h, a, kernel, f_self, f_other, out):
         engines = {mybir.EngineType.PE, mybir.EngineType.DVE, mybir.EngineType.Activation, mybir.EngineType.Pool}
         with tc.manual_schedule(engines=engines):
             for blk in range(TILES // 4):
-                mask_part(psum_dense, "dense", 0, blk)
+                turn_adj(psum_dense, "dense", 0, blk)
+                make_mask(0, blk)
             make_weight(0)
             turn_fs(0)
+            negate_fs(0)
             for blk in range(TILES // 4):
                 turn_fo(0, blk, nc.vector.tensor_copy)
-            for q in range(CHUNKS):
-                dense(0, q)
+            for first in (0, 2):
+                dense(0, first)
+            turn_adj(psum_mask, "zt", 1, 0)
+            make_mask(1, 0)
             waiting = []
             finished = 0
             for step in range(UNITS + 4):
                 tile_no, hd = divmod(step, H)
                 live = step < UNITS
+                ahead = step + H + 1
                 if hd == 0 and tile_no + 2 < TILES:
                     load_adj(tile_no + 2)
                     if tile_no % 2 == 0:
                         load_fs(tile_no // 2 + 1)
+                if live:
+                    weigh(step, 0)
+                if hd == 2 and tile_no + 1 < TILES:
+                    negate_fs(tile_no + 1)
+                if ahead < UNITS:
+                    turn_adj(psum_mask, "zt", ahead // H, ahead % H)
                 if step + 1 < H:
                     for blk in range(TILES // 4):
                         turn_fo(step + 1, blk, nc.scalar.copy)
+                if 0 <= step - 3 < UNITS:
+                    group(step - 3, 0)
+                    group(step - 3, 1)
+                if live:
+                    weigh(step, 1)
+                if step + 1 < UNITS:
+                    dense(step + 1, 0)
                 if step == 7:
                     mark_padding()
-                for q in range(CHUNKS):
-                    if live:
-                        weigh(step, q)
-                    if step + 1 < UNITS:
-                        dense(step + 1, q)
-                    if q == 1 and 0 <= step - 1 < UNITS:
-                        bend_min(step - 1)
-                    if q == 2 and 0 <= step - 1 < UNITS:
-                        shift_min(step - 1)
-                    if hd == 3 and step >= 2 * H - 1 and q < 3:
-                        gain_step(tile_no - 1, q)
-                    if q == 0 and 0 <= step - 3 < UNITS:
-                        group(step - 3, 0)
-                        group(step - 3, 1)
-                    if q == 1 and 0 <= step - FEATS_START < PASSES:
-                        make_feats(step - FEATS_START, 0)
-                        make_feats(step - FEATS_START, 1)
+                if 0 <= step - 1 < UNITS:
+                    bend_min(step - 1)
+                if hd == 3 and step >= 2 * H - 1:
+                    gain_step(tile_no - 1, 0)
+                if 0 <= step - FEATS_START < PASSES:
+                    make_feats(step - FEATS_START, 0)
+                    make_feats(step - FEATS_START, 1)
                 if live:
-                    bend(step)
+                    weigh(step, 2)
+                    bend(step, OWN, 3 * BANK)
+                if 0 <= step - 1 < UNITS:
+                    shift_min(step - 1)
+                if hd == 3 and step >= 2 * H - 1:
+                    gain_step(tile_no - 1, 1)
+                if live:
+                    weigh(step, 3)
+                if step + 1 < UNITS:
+                    dense(step + 1, 2)
+                if live:
+                    bend(step, 3 * BANK, N)
+                if ahead < UNITS:
+                    make_mask(ahead // H, ahead % H)
+                if hd == 3 and step >= 2 * H - 1:
+                    gain_step(tile_no - 1, 2)
                 if live:
                     bend_own(step)
                 if live and hd == 2 and tile_no + 1 < TILES:
@@ -468,7 +504,6 @@ def tile_gatlayersinglebatch_pa_kernel(tc, h, a, kernel, f_self, f_other, out):
                     quantise_x(step - 3)
                 if 0 <= step - 3 < PASSES:
                     find_zeros(step - 3)
-                    count_zeros(step - 3)
                 if 0 <= step - FEATS_START - 1 < PASSES:
                     quantise_feats(step - FEATS_START - 1)
                 if live:
@@ -478,18 +513,17 @@ def tile_gatlayersinglebatch_pa_kernel(tc, h, a, kernel, f_self, f_other, out):
                 if 0 <= step - FEATS_START < PASSES:
                     make_feats(step - FEATS_START, 2)
                     make_feats(step - FEATS_START, 3)
-                for ahead in range(step + H if step == 0 else step + H + 1, step + H + 2):
-                    if ahead < UNITS:
-                        mask_part(psum_mask, "zt", ahead // H, ahead % H)
-                        if ahead % H == 2:
-                            turn_fs(ahead // H)
+                if 0 <= step - 2 < UNITS:
+                    turn(step - 2)
+                if 0 <= step - 3 < PASSES:
+                    count_zeros(step - 3)
                 ready = step > FEATS_START + PASSES
                 units = [unit for unit in waiting[:2] if ready and unit // H == finished]
                 waiting = waiting[len(units) :]
                 for unit in units:
                     aggregate(unit)
-                if 0 <= step - 2 < UNITS:
-                    turn(step - 2)
+                if hd == 1 and tile_no + 1 < TILES:
+                    turn_fs(tile_no + 1)
                 if units and units[-1] % H == H - 1:
                     finish(finished)
                     finished += 1

@@ -32,9 +32,9 @@ SCALE = 1.0 / math.sqrt(D)
 NO_EDGE_LOG = 69.0
 EDGE_SLOPE = 2.0**112
 LEAST_WEIGHT = 2.0**-60
-OWN = 512
+OWN = 576
 CEILING = 2.0**30
-FEATS_START = 4
+FEATS_START = 6
 TINY = 1.0e-30
 
 FLOPS = 2 * N * F * H * O + 2 * H * N * N * D + 2 * H * N * N * O
@@ -56,8 +56,8 @@ def tile_gatlayersinglebatch_pa_kernel(tc, h, a, kernel, f_self, f_other, out):
         maskp = ctx.enter_context(tc.tile_pool(name="maskp", bufs=2))
         tp = ctx.enter_context(tc.tile_pool(name="t", bufs=2))
         zp = ctx.enter_context(tc.tile_pool(name="z", bufs=2))
-        emp = ctx.enter_context(tc.tile_pool(name="em", bufs=3))
-        codep = ctx.enter_context(tc.tile_pool(name="codes", bufs=8))
+        emp = ctx.enter_context(tc.tile_pool(name="em", bufs=2))
+        codep = ctx.enter_context(tc.tile_pool(name="codes", bufs=12))
         small = ctx.enter_context(tc.tile_pool(name="small", bufs=3))
         outp = ctx.enter_context(tc.tile_pool(name="outp", bufs=2))
         psum_dense = ctx.enter_context(tc.psum_pool(name="psum_dense", bufs=4))
@@ -77,13 +77,16 @@ def tile_gatlayersinglebatch_pa_kernel(tc, h, a, kernel, f_self, f_other, out):
         foT = const.tile([P, H, N], BF16)
         fo_raw_of = {}
 
-        def load_fo(hd):
+        def load_fo(hd, parts):
             fo_raw = raw.tile([P, TILES, D], BF16, tag="fo_raw")
-            nc.sync.dma_start(out=fo_raw[:], in_=f_other[hd, :, :].rearrange("(t p) d -> p t d", p=P))
+            rows = f_other[hd, :, :].rearrange("(t p) d -> p t d", p=P)
+            for part in range(parts):
+                tiles = slice(part * TILES // parts, (part + 1) * TILES // parts)
+                nc.sync.dma_start(out=fo_raw[:, tiles, :], in_=rows[:, tiles, :])
             fo_raw_of[hd] = fo_raw
 
-        def turn_fo(hd, blk, copy):
-            pt = psum_tr.tile([P, 4, P], BF16, tag="tr")
+        def turn_fo(hd, blk, psum, tag, copy):
+            pt = psum.tile([P, 4, P], BF16, tag=tag)
             for k in range(4):
                 nc.tensor.transpose(pt[:, k, :], fo_raw_of[hd][:, 4 * blk + k, :], ident_bf[:])
             copy(out=foT[:, hd, blk * BANK : (blk + 1) * BANK], in_=pt[:].rearrange("p k n -> p (k n)"))
@@ -121,6 +124,9 @@ def tile_gatlayersinglebatch_pa_kernel(tc, h, a, kernel, f_self, f_other, out):
                     in_=kernel[hd, :, :].rearrange("(u p e) o -> p u e o", u=2, e=2),
                 )
 
+        def group_kernel():
+            nc.vector.tensor_copy(out=k_grp[:], in_=k_raw[:].rearrange("p h t o -> p h o t"))
+
         def quantise_kernel():
             nc.vector.quantize_mx(
                 out=k_codes[:].bitcast(FP8X4), scales=k_scales[:], in_=k_grp[:].rearrange("p h o t -> p (h o t)")
@@ -131,6 +137,7 @@ def tile_gatlayersinglebatch_pa_kernel(tc, h, a, kernel, f_self, f_other, out):
         x_grp32 = x_grp[:].bitcast(F32).rearrange("p (t n u) -> p t n u", t=TILES, u=2)
         x_codes = setup.tile([P, TILES * P], U32, align_bytes=64)
         x_scales = setup.tile([P, TILES * P], U8, align_bytes=64)
+        xt_of = {}
         zero_of = {}
         count_of = []
         rowmask = const.tile([P, TILES], F32)
@@ -145,8 +152,11 @@ def tile_gatlayersinglebatch_pa_kernel(tc, h, a, kernel, f_self, f_other, out):
                 words = x_raw[:, pair, e, :].bitcast(F32)
                 for u in range(2):
                     nc.tensor.transpose(xt[:, e, u, :], words[:, u * P : (u + 1) * P], ident_f32[:])
-            nc.vector.tensor_copy(
-                out=x_grp32[:, 2 * pair : 2 * pair + 2, :, :], in_=xt[:].rearrange("p t u n -> p t n u")
+            xt_of[pair] = xt
+
+        def group_x(pair):
+            nc.scalar.copy(
+                out=x_grp32[:, 2 * pair : 2 * pair + 2, :, :], in_=xt_of[pair][:].rearrange("p t u n -> p t n u")
             )
 
         def quantise_x(half):
@@ -186,6 +196,7 @@ def tile_gatlayersinglebatch_pa_kernel(tc, h, a, kernel, f_self, f_other, out):
             nc.vector.tensor_single_scalar(out=rowmask[:], in_=count_of[0][:], scalar=float(F), op=ALU.is_lt)
 
         f_grp_of = []
+        fb_of = {}
         f_codes = const.tile([P, PASSES, H, O], U32, align_bytes=64)
         f_scales = const.tile([P, PASSES, H, O], U8, align_bytes=64)
 
@@ -205,7 +216,10 @@ def tile_gatlayersinglebatch_pa_kernel(tc, h, a, kernel, f_self, f_other, out):
                     start=True,
                     stop=True,
                 )
-            nc.scalar.copy(out=f_grp_of[0][:, g, hd, :, :], in_=fb[:].rearrange("p t o -> p o t"))
+            fb_of[g, hd] = fb
+
+        def group_feats(g, hd):
+            nc.scalar.copy(out=f_grp_of[0][:, g, hd, :, :], in_=fb_of[g, hd][:].rearrange("p t o -> p o t"))
 
         def quantise_feats(g):
             nc.vector.quantize_mx(
@@ -217,7 +231,6 @@ def tile_gatlayersinglebatch_pa_kernel(tc, h, a, kernel, f_self, f_other, out):
         adj_of = {}
         zt_of = {}
         mask_of = {}
-        weight_of = {}
         banks_of = {}
         t_of = {}
         z_of = {}
@@ -232,15 +245,12 @@ def tile_gatlayersinglebatch_pa_kernel(tc, h, a, kernel, f_self, f_other, out):
         gain_of = {}
         acc_of = {}
 
-        def load_adj(tile_no):
+        def load_adj(tile_no, parts):
             adj_t = adjp.tile([P, N], BF16, tag="adj")
-            nc.sync.dma_start(out=adj_t[:], in_=adj_rows[tile_no // 2, tile_no % 2])
+            for part in range(parts):
+                cols = slice(part * N // parts, (part + 1) * N // parts)
+                nc.sync.dma_start(out=adj_t[:, cols], in_=adj_rows[tile_no // 2, tile_no % 2][:, cols])
             adj_of[tile_no] = adj_t
-
-        def make_weight(tile_no):
-            weight = maskp.tile([P, N], BF16, tag="weight")
-            nc.vector.tensor_scalar_max(out=weight[:], in0=adj_of[tile_no][:], scalar1=LEAST_WEIGHT)
-            weight_of[tile_no] = weight
 
         def turn_adj(psum, tag, tile_no, blk):
             adj_t = adj_of[tile_no]
@@ -261,9 +271,9 @@ def tile_gatlayersinglebatch_pa_kernel(tc, h, a, kernel, f_self, f_other, out):
                 scale=-EDGE_SLOPE,
             )
 
-        def dense(i, first):
+        def dense(i, banks):
             tile_no, hd = divmod(i, H)
-            for q in (first, first + 1):
+            for q in banks:
                 bank = psum_dense.tile([P, BANK], F32, tag="dense")
                 nc.tensor.matmul(
                     bank[:],
@@ -273,7 +283,7 @@ def tile_gatlayersinglebatch_pa_kernel(tc, h, a, kernel, f_self, f_other, out):
                     stop=False,
                 )
                 banks_of[i, q] = bank
-            for q in (first, first + 1):
+            for q in banks:
                 for k in range(4):
                     nc.tensor.matmul(
                         banks_of[i, q][:, k * P : (k + 1) * P],
@@ -289,8 +299,13 @@ def tile_gatlayersinglebatch_pa_kernel(tc, h, a, kernel, f_self, f_other, out):
                 t = tp.tile([P, N], F32, tag="t")
                 t_of[i] = t
             cols = slice(q * BANK, (q + 1) * BANK)
-            nc.vector.tensor_tensor(
-                out=t_of[i][:, cols], in0=banks_of[i, q][:], in1=weight_of[i // H][:, cols], op=ALU.mult
+            nc.vector.scalar_tensor_tensor(
+                out=t_of[i][:, cols],
+                in0=adj_of[i // H][:, cols],
+                scalar=LEAST_WEIGHT,
+                in1=banks_of[i, q][:],
+                op0=ALU.max,
+                op1=ALU.mult,
             )
 
         def bend(i, first, last):
@@ -412,14 +427,14 @@ def tile_gatlayersinglebatch_pa_kernel(tc, h, a, kernel, f_self, f_other, out):
                 )
             nc.sync.dma_start(out=out_rows[tile_no // 2, tile_no % 2], in_=o_sb[:].rearrange("p h o -> p (h o)"))
 
-        load_adj(0)
-        load_fo(0)
+        load_adj(0, 2)
         load_fs(0)
-        load_fo(1)
-        load_adj(1)
+        load_fo(0, 2)
+        load_fo(1, 1)
+        load_adj(1, 1)
+        load_fo(2, 1)
+        load_fo(3, 1)
         load_kernel()
-        load_fo(2)
-        load_fo(3)
         for part in range(TILES // 4):
             load_x(part)
         engines = {mybir.EngineType.PE, mybir.EngineType.DVE, mybir.EngineType.Activation, mybir.EngineType.Pool}
@@ -427,15 +442,18 @@ def tile_gatlayersinglebatch_pa_kernel(tc, h, a, kernel, f_self, f_other, out):
             for blk in range(TILES // 4):
                 turn_adj(psum_dense, "dense", 0, blk)
                 make_mask(0, blk)
-            make_weight(0)
             turn_fs(0)
             negate_fs(0)
             for blk in range(TILES // 4):
-                turn_fo(0, blk, nc.vector.tensor_copy)
-            for first in (0, 2):
-                dense(0, first)
-            turn_adj(psum_mask, "zt", 1, 0)
-            make_mask(1, 0)
+                if blk == 2:
+                    turn_fo(0, blk, psum_acc, "acc", nc.vector.tensor_copy)
+                else:
+                    turn_fo(0, blk, psum_tr, "tr", nc.vector.tensor_copy)
+            for q in range(CHUNKS):
+                dense(0, (q,))
+                if q % 2 == 1:
+                    turn_fo(1, q - 1, psum_tr, "tr", nc.scalar.copy)
+                    turn_fo(1, q, psum_tr, "tr", nc.scalar.copy)
             waiting = []
             finished = 0
             for step in range(UNITS + 4):
@@ -443,34 +461,35 @@ def tile_gatlayersinglebatch_pa_kernel(tc, h, a, kernel, f_self, f_other, out):
                 live = step < UNITS
                 ahead = step + H + 1
                 if hd == 0 and tile_no + 2 < TILES:
-                    load_adj(tile_no + 2)
+                    load_adj(tile_no + 2, 1)
                     if tile_no % 2 == 0:
                         load_fs(tile_no // 2 + 1)
                 if live:
                     weigh(step, 0)
-                if hd == 2 and tile_no + 1 < TILES:
+                if hd == 3 and tile_no + 1 < TILES:
                     negate_fs(tile_no + 1)
-                if ahead < UNITS:
+                if ahead < UNITS and step > 0:
                     turn_adj(psum_mask, "zt", ahead // H, ahead % H)
-                if step + 1 < H:
-                    for blk in range(TILES // 4):
-                        turn_fo(step + 1, blk, nc.scalar.copy)
                 if 0 <= step - 3 < UNITS:
                     group(step - 3, 0)
                     group(step - 3, 1)
                 if live:
                     weigh(step, 1)
                 if step + 1 < UNITS:
-                    dense(step + 1, 0)
+                    dense(step + 1, (0, 1))
                 if step == 7:
                     mark_padding()
                 if 0 <= step - 1 < UNITS:
                     bend_min(step - 1)
                 if hd == 3 and step >= 2 * H - 1:
                     gain_step(tile_no - 1, 0)
-                if 0 <= step - FEATS_START < PASSES:
-                    make_feats(step - FEATS_START, 0)
-                    make_feats(step - FEATS_START, 1)
+                if 2 <= step < 2 + TILES // 4:
+                    turn_x(2 * step - 4)
+                    turn_x(2 * step - 3)
+                feats = divmod(step - FEATS_START, 2)
+                if 0 <= feats[0] < PASSES:
+                    make_feats(feats[0], 2 * feats[1])
+                    make_feats(feats[0], 2 * feats[1] + 1)
                 if live:
                     weigh(step, 2)
                     bend(step, OWN, 3 * BANK)
@@ -481,48 +500,53 @@ def tile_gatlayersinglebatch_pa_kernel(tc, h, a, kernel, f_self, f_other, out):
                 if live:
                     weigh(step, 3)
                 if step + 1 < UNITS:
-                    dense(step + 1, 2)
+                    dense(step + 1, (2, 3))
+                if 2 <= step < 2 + TILES // 4:
+                    group_x(2 * step - 4)
+                    group_x(2 * step - 3)
+                if 0 <= feats[0] < PASSES:
+                    group_feats(feats[0], 2 * feats[1])
+                    group_feats(feats[0], 2 * feats[1] + 1)
                 if live:
                     bend(step, 3 * BANK, N)
+                if step == 0:
+                    turn_adj(psum_mask, "zt", 1, 0)
+                    make_mask(1, 0)
+                    turn_adj(psum_mask, "zt", 1, 1)
                 if ahead < UNITS:
                     make_mask(ahead // H, ahead % H)
+                if step < 2:
+                    for blk in range(TILES // 4):
+                        turn_fo(step + 2, blk, psum_tr, "tr", nc.scalar.copy)
                 if hd == 3 and step >= 2 * H - 1:
                     gain_step(tile_no - 1, 2)
                 if live:
                     bend_own(step)
-                if live and hd == 2 and tile_no + 1 < TILES:
-                    make_weight(tile_no + 1)
+                if step == 1:
+                    group_kernel()
+                if step == 2:
+                    quantise_kernel()
                 if 0 <= step - 4 < UNITS:
                     quantise(step - 4)
                     waiting.append(step - 4)
-                if step == 0:
-                    nc.vector.tensor_copy(out=k_grp[:], in_=k_raw[:].rearrange("p h t o -> p h o t"))
-                if step in (1, 2):
-                    for pair in range(4):
-                        turn_x(4 * (step - 1) + pair)
-                if step in (3, 4):
-                    quantise_x(step - 3)
-                if 0 <= step - 3 < PASSES:
+                if step in (4, 7):
+                    quantise_x((step - 4) // 3)
+                if 3 <= step < 3 + PASSES:
                     find_zeros(step - 3)
-                if 0 <= step - FEATS_START - 1 < PASSES:
-                    quantise_feats(step - FEATS_START - 1)
+                if 0 < step - FEATS_START <= 2 * PASSES and (step - FEATS_START) % 2 == 0:
+                    quantise_feats((step - FEATS_START) // 2 - 1)
                 if live:
                     row_min(step)
-                if step == 0:
-                    quantise_kernel()
-                if 0 <= step - FEATS_START < PASSES:
-                    make_feats(step - FEATS_START, 2)
-                    make_feats(step - FEATS_START, 3)
-                if 0 <= step - 2 < UNITS:
-                    turn(step - 2)
-                if 0 <= step - 3 < PASSES:
+                if 3 <= step < 3 + PASSES:
                     count_zeros(step - 3)
-                ready = step > FEATS_START + PASSES
+                ready = step > FEATS_START + 2 * PASSES
                 units = [unit for unit in waiting[:2] if ready and unit // H == finished]
                 waiting = waiting[len(units) :]
                 for unit in units:
                     aggregate(unit)
-                if hd == 1 and tile_no + 1 < TILES:
+                if 0 <= step - 2 < UNITS:
+                    turn(step - 2)
+                if hd == 2 and tile_no + 1 < TILES:
                     turn_fs(tile_no + 1)
                 if units and units[-1] % H == H - 1:
                     finish(finished)

@@ -32,7 +32,8 @@ SCALE = 1.0 / math.sqrt(D)
 NO_EDGE_LOG = 69.0
 EDGE_SLOPE = 2.0**112
 LEAST_WEIGHT = 2.0**-60
-OWN = 576
+OWN = 512
+LAST_OWN = 1152
 CEILING = 2.0**30
 FEATS_START = 6
 TINY = 1.0e-30
@@ -55,7 +56,7 @@ def tile_gatlayersinglebatch_pa_kernel(tc, h, a, kernel, f_self, f_other, out):
         adjp = ctx.enter_context(tc.tile_pool(name="adj", bufs=3))
         maskp = ctx.enter_context(tc.tile_pool(name="maskp", bufs=2))
         tp = ctx.enter_context(tc.tile_pool(name="t", bufs=2))
-        zp = ctx.enter_context(tc.tile_pool(name="z", bufs=2))
+        zp = ctx.enter_context(tc.tile_pool(name="z", bufs=3))
         emp = ctx.enter_context(tc.tile_pool(name="em", bufs=2))
         codep = ctx.enter_context(tc.tile_pool(name="codes", bufs=12))
         small = ctx.enter_context(tc.tile_pool(name="small", bufs=3))
@@ -308,20 +309,23 @@ def tile_gatlayersinglebatch_pa_kernel(tc, h, a, kernel, f_self, f_other, out):
                 op1=ALU.mult,
             )
 
+        def own_cols(i):
+            return LAST_OWN if i == UNITS - 1 else OWN
+
         def bend(i, first, last):
             t = t_of[i]
-            if first == OWN:
+            if first == own_cols(i):
                 z = zp.tile([P, N], F32, tag="z")
                 z_of[i] = z
             cols = slice(first, last)
             nc.scalar.activation(out=z_of[i][:, cols], in_=t[:, cols], func=ACT.Relu, scale=1.0 - SLOPE)
             if last == N:
-                cols = slice(OWN, N)
+                cols = slice(own_cols(i), N)
                 nc.gpsimd.tensor_tensor(out=z_of[i][:, cols], in0=t[:, cols], in1=z_of[i][:, cols], op=ALU.subtract)
 
         def bend_own(i):
             t = t_of[i]
-            own = slice(0, OWN)
+            own = slice(0, own_cols(i))
             nc.vector.scalar_tensor_tensor(
                 out=z_of[i][:, own], in0=t[:, own], scalar=SLOPE, in1=t[:, own], op0=ALU.mult, op1=ALU.min
             )
@@ -372,14 +376,17 @@ def tile_gatlayersinglebatch_pa_kernel(tc, h, a, kernel, f_self, f_other, out):
                         nc.tensor.transpose(tr[:, gg, u, :], words[:, first : first + P], ident_f32[:])
                 tr_of[i, half] = tr
 
-        def group(i, half):
+        def group(i, half, drain):
             if half == 0:
                 grp = emp.tile([P, N], BF16, tag="grp", align_bytes=64)
                 grp_of[i] = grp
             grp32 = grp_of[i][:].bitcast(F32).rearrange("p (g n u) -> p g n u", g=PASSES, u=2)
             dst = grp32[:, 2 * half : 2 * half + 2, :, :]
             src = tr_of[i, half][:].rearrange("p g u n -> p g n u")
-            nc.scalar.copy(out=dst, in_=src)
+            if half == 1 and drain:
+                nc.vector.tensor_copy(out=dst, in_=src)
+            else:
+                nc.scalar.copy(out=dst, in_=src)
 
         def quantise(i):
             codes = codep.tile([P, PASSES * P], U32, tag="codes", align_bytes=64)
@@ -460,6 +467,7 @@ def tile_gatlayersinglebatch_pa_kernel(tc, h, a, kernel, f_self, f_other, out):
                 tile_no, hd = divmod(step, H)
                 live = step < UNITS
                 ahead = step + H + 1
+                gain_now = tile_no > 0 and hd == (3 if live else 2)
                 if hd == 0 and tile_no + 2 < TILES:
                     load_adj(tile_no + 2, 1)
                     if tile_no % 2 == 0:
@@ -470,9 +478,9 @@ def tile_gatlayersinglebatch_pa_kernel(tc, h, a, kernel, f_self, f_other, out):
                     negate_fs(tile_no + 1)
                 if ahead < UNITS and step > 0:
                     turn_adj(psum_mask, "zt", ahead // H, ahead % H)
-                if 0 <= step - 3 < UNITS:
-                    group(step - 3, 0)
-                    group(step - 3, 1)
+                if 0 <= step - 3 < UNITS and live:
+                    group(step - 3, 0, not live)
+                    group(step - 3, 1, not live)
                 if live:
                     weigh(step, 1)
                 if step + 1 < UNITS:
@@ -481,7 +489,7 @@ def tile_gatlayersinglebatch_pa_kernel(tc, h, a, kernel, f_self, f_other, out):
                     mark_padding()
                 if 0 <= step - 1 < UNITS:
                     bend_min(step - 1)
-                if hd == 3 and step >= 2 * H - 1:
+                if gain_now:
                     gain_step(tile_no - 1, 0)
                 if 2 <= step < 2 + TILES // 4:
                     turn_x(2 * step - 4)
@@ -492,13 +500,19 @@ def tile_gatlayersinglebatch_pa_kernel(tc, h, a, kernel, f_self, f_other, out):
                     make_feats(feats[0], 2 * feats[1] + 1)
                 if live:
                     weigh(step, 2)
-                    bend(step, OWN, 3 * BANK)
+                    bend(step, own_cols(step), 3 * BANK)
                 if 0 <= step - 1 < UNITS:
                     shift_min(step - 1)
-                if hd == 3 and step >= 2 * H - 1:
+                if gain_now:
                     gain_step(tile_no - 1, 1)
                 if live:
                     weigh(step, 3)
+                if 0 <= step - 4 < UNITS and not live:
+                    quantise(step - 4)
+                    waiting.append(step - 4)
+                if 0 <= step - 3 < UNITS and not live:
+                    group(step - 3, 0, not live)
+                    group(step - 3, 1, not live)
                 if step + 1 < UNITS:
                     dense(step + 1, (2, 3))
                 if 2 <= step < 2 + TILES // 4:
@@ -518,17 +532,17 @@ def tile_gatlayersinglebatch_pa_kernel(tc, h, a, kernel, f_self, f_other, out):
                 if step < 2:
                     for blk in range(TILES // 4):
                         turn_fo(step + 2, blk, psum_tr, "tr", nc.scalar.copy)
-                if hd == 3 and step >= 2 * H - 1:
+                if gain_now:
                     gain_step(tile_no - 1, 2)
+                if 0 <= step - 4 < UNITS and live:
+                    quantise(step - 4)
+                    waiting.append(step - 4)
                 if live:
                     bend_own(step)
                 if step == 1:
                     group_kernel()
                 if step == 2:
                     quantise_kernel()
-                if 0 <= step - 4 < UNITS:
-                    quantise(step - 4)
-                    waiting.append(step - 4)
                 if step in (4, 7):
                     quantise_x((step - 4) // 3)
                 if 3 <= step < 3 + PASSES:

@@ -35,6 +35,7 @@ LEAST_WEIGHT = 2.0**-60
 OWN = 512
 LAST_OWN = 1152
 CEILING = 2.0**30
+PLAIN_BANKS = 7
 FEATS_START = 6
 TINY = 1.0e-30
 
@@ -51,7 +52,8 @@ def tile_gatlayersinglebatch_pa_kernel(tc, h, a, kernel, f_self, f_other, out):
         const = ctx.enter_context(tc.tile_pool(name="const", bufs=1))
         setup = ctx.enter_context(tc.tile_pool(name="setup", bufs=1))
         raw = ctx.enter_context(tc.tile_pool(name="raw", bufs=4))
-        zerop = ctx.enter_context(tc.tile_pool(name="zerop", bufs=2))
+        zerop = ctx.enter_context(tc.tile_pool(name="zerop", bufs=1))
+        edgep = ctx.enter_context(tc.tile_pool(name="edgep", bufs=2))
         fsp = ctx.enter_context(tc.tile_pool(name="fs", bufs=2))
         adjp = ctx.enter_context(tc.tile_pool(name="adj", bufs=3))
         maskp = ctx.enter_context(tc.tile_pool(name="maskp", bufs=2))
@@ -72,6 +74,8 @@ def tile_gatlayersinglebatch_pa_kernel(tc, h, a, kernel, f_self, f_other, out):
         masks.make_identity(nc, ident_f32[:])
         log_bias = const.tile([P, 1], F32)
         nc.vector.memset(log_bias[:], NO_EDGE_LOG)
+        big = const.tile([P, P], BF16)
+        nc.vector.tensor_scalar_mul(out=big[:], in0=ident_bf[:], scalar1=2.0**100)
         ones = const.tile([P, 1], BF16)
         nc.vector.memset(ones[:], 1.0)
 
@@ -230,6 +234,7 @@ def tile_gatlayersinglebatch_pa_kernel(tc, h, a, kernel, f_self, f_other, out):
             )
 
         adj_of = {}
+        is_zero_of = {}
         zt_of = {}
         mask_of = {}
         banks_of = {}
@@ -253,6 +258,15 @@ def tile_gatlayersinglebatch_pa_kernel(tc, h, a, kernel, f_self, f_other, out):
                 nc.sync.dma_start(out=adj_t[:, cols], in_=adj_rows[tile_no // 2, tile_no % 2][:, cols])
             adj_of[tile_no] = adj_t
 
+        def find_no_edge(tile_no, first, last):
+            if first == 0:
+                is_zero = edgep.tile([P, N], BF16, tag="is_zero")
+                is_zero_of[tile_no] = is_zero
+            cols = slice(first * BANK, last * BANK)
+            nc.vector.tensor_single_scalar(
+                out=is_zero_of[tile_no][:, cols], in_=adj_of[tile_no][:, cols], scalar=0.0, op=ALU.is_equal
+            )
+
         def turn_adj(psum, tag, tile_no, blk):
             adj_t = adj_of[tile_no]
             zt = psum.tile([P, 4, P], BF16, tag=tag)
@@ -261,7 +275,7 @@ def tile_gatlayersinglebatch_pa_kernel(tc, h, a, kernel, f_self, f_other, out):
             zt_of[tile_no, blk] = zt
 
         def make_mask(tile_no, blk):
-            if blk == 0:
+            if tile_no not in mask_of:
                 maskT = maskp.tile([P, TILES, P], F32, tag="maskT")
                 mask_of[tile_no] = maskT
             nc.scalar.activation(
@@ -285,6 +299,12 @@ def tile_gatlayersinglebatch_pa_kernel(tc, h, a, kernel, f_self, f_other, out):
                 )
                 banks_of[i, q] = bank
             for q in banks:
+                if CHUNKS * tile_no + q < PLAIN_BANKS:
+                    cols = slice(q * BANK, (q + 1) * BANK)
+                    nc.tensor.matmul(
+                        banks_of[i, q][:], lhsT=big[:], rhs=is_zero_of[tile_no][:, cols], start=False, stop=True
+                    )
+                    continue
                 for k in range(4):
                     nc.tensor.matmul(
                         banks_of[i, q][:, k * P : (k + 1) * P],
@@ -434,9 +454,9 @@ def tile_gatlayersinglebatch_pa_kernel(tc, h, a, kernel, f_self, f_other, out):
                 )
             nc.sync.dma_start(out=out_rows[tile_no // 2, tile_no % 2], in_=o_sb[:].rearrange("p h o -> p (h o)"))
 
-        load_adj(0, 2)
-        load_fs(0)
         load_fo(0, 2)
+        load_fs(0)
+        load_adj(0, 2)
         load_fo(1, 1)
         load_adj(1, 1)
         load_fo(2, 1)
@@ -447,15 +467,14 @@ def tile_gatlayersinglebatch_pa_kernel(tc, h, a, kernel, f_self, f_other, out):
         engines = {mybir.EngineType.PE, mybir.EngineType.DVE, mybir.EngineType.Activation, mybir.EngineType.Pool}
         with tc.manual_schedule(engines=engines):
             for blk in range(TILES // 4):
-                turn_adj(psum_dense, "dense", 0, blk)
-                make_mask(0, blk)
-            turn_fs(0)
-            negate_fs(0)
-            for blk in range(TILES // 4):
                 if blk == 2:
                     turn_fo(0, blk, psum_acc, "acc", nc.vector.tensor_copy)
                 else:
                     turn_fo(0, blk, psum_tr, "tr", nc.vector.tensor_copy)
+            turn_fs(0)
+            negate_fs(0)
+            find_no_edge(0, 0, 2)
+            find_no_edge(0, 2, 4)
             for q in range(CHUNKS):
                 dense(0, (q,))
                 if q % 2 == 1:
@@ -476,7 +495,7 @@ def tile_gatlayersinglebatch_pa_kernel(tc, h, a, kernel, f_self, f_other, out):
                     weigh(step, 0)
                 if hd == 3 and tile_no + 1 < TILES:
                     negate_fs(tile_no + 1)
-                if ahead < UNITS and step > 0:
+                if PLAIN_BANKS <= ahead < UNITS:
                     turn_adj(psum_mask, "zt", ahead // H, ahead % H)
                 if 0 <= step - 3 < UNITS and live:
                     group(step - 3, 0, not live)
@@ -523,11 +542,7 @@ def tile_gatlayersinglebatch_pa_kernel(tc, h, a, kernel, f_self, f_other, out):
                     group_feats(feats[0], 2 * feats[1] + 1)
                 if live:
                     bend(step, 3 * BANK, N)
-                if step == 0:
-                    turn_adj(psum_mask, "zt", 1, 0)
-                    make_mask(1, 0)
-                    turn_adj(psum_mask, "zt", 1, 1)
-                if ahead < UNITS:
+                if PLAIN_BANKS <= ahead < UNITS:
                     make_mask(ahead // H, ahead % H)
                 if step < 2:
                     for blk in range(TILES // 4):
@@ -539,6 +554,8 @@ def tile_gatlayersinglebatch_pa_kernel(tc, h, a, kernel, f_self, f_other, out):
                     waiting.append(step - 4)
                 if live:
                     bend_own(step)
+                if step == 0:
+                    find_no_edge(1, 0, PLAIN_BANKS - CHUNKS)
                 if step == 1:
                     group_kernel()
                 if step == 2:
@@ -562,8 +579,8 @@ def tile_gatlayersinglebatch_pa_kernel(tc, h, a, kernel, f_self, f_other, out):
                     turn(step - 2)
                 if hd == 2 and tile_no + 1 < TILES:
                     turn_fs(tile_no + 1)
+                if 0 <= step - 1 < UNITS:
+                    exponential(step - 1)
                 if units and units[-1] % H == H - 1:
                     finish(finished)
                     finished += 1
-                if 0 <= step - 1 < UNITS:
-                    exponential(step - 1)

from contextlib import ExitStack
import math

import concourse.masks as masks
import concourse.mybir as mybir

F32 = mybir.dt.float32
BF16 = mybir.dt.bfloat16
U32 = mybir.dt.uint32
U8 = mybir.dt.uint8
FP8X4 = mybir.dt.float8_e4m3fn_x4
ALU = mybir.AluOpType
ACT = mybir.ActivationFunctionType
AX = mybir.AxisListType

P = 128
N = 2048
F = 512
H = 4
O = 128
D = 128
PACK = 4
K_PASS = P * PACK
TILES = N // P
PASSES = N // K_PASS
BANK = 512
CHUNKS = N // BANK
UNITS = TILES * H

SLOPE = 0.2
SCALE = 1.0 / math.sqrt(D)
NO_EDGE_LOG = 69.0
EDGE_SLOPE = 2.0**112
LEAST_WEIGHT = 2.0**-60
OWN = 512
LAST_OWN = 1152
CEILING = 2.0**30
PLAIN_BANKS = 7
FEATS_START = 6
TINY = 1.0e-30

FLOPS = 2 * N * F * H * O + 2 * H * N * N * D + 2 * H * N * N * O


def tile_gatlayersinglebatch_pa_kernel(tc, h, a, kernel, f_self, f_other, out):
    nc = tc.nc
    x_rows = h.rearrange("b (c p e) f -> p (b c) e f", p=P, e=2)
    adj_rows = a.rearrange("b (c p e) j -> (b c) e p j", p=P, e=2)
    out_rows = out.rearrange("b (c p e) k -> (b c) e p k", p=P, e=2)

    with ExitStack() as ctx:
        const = ctx.enter_context(tc.tile_pool(name="const", bufs=1))
        setup = ctx.enter_context(tc.tile_pool(name="setup", bufs=1))
        raw = ctx.enter_context(tc.tile_pool(name="raw", bufs=4))
        zerop = ctx.enter_context(tc.tile_pool(name="zerop", bufs=1))
        edgep = ctx.enter_context(tc.tile_pool(name="edgep", bufs=2))
        fsp = ctx.enter_context(tc.tile_pool(name="fs", bufs=2))
        adjp = ctx.enter_context(tc.tile_pool(name="adj", bufs=3))
        maskp = ctx.enter_context(tc.tile_pool(name="maskp", bufs=2))
        tp = ctx.enter_context(tc.tile_pool(name="t", bufs=2))
        zp = ctx.enter_context(tc.tile_pool(name="z", bufs=3))
        emp = ctx.enter_context(tc.tile_pool(name="em", bufs=2))
        codep = ctx.enter_context(tc.tile_pool(name="codes", bufs=12))
        small = ctx.enter_context(tc.tile_pool(name="small", bufs=3))
        outp = ctx.enter_context(tc.tile_pool(name="outp", bufs=2))
        psum_dense = ctx.enter_context(tc.psum_pool(name="psum_dense", bufs=4))
        psum_tr = ctx.enter_context(tc.psum_pool(name="psum_tr", bufs=2))
        psum_mask = ctx.enter_context(tc.psum_pool(name="psum_mask", bufs=1))
        psum_acc = ctx.enter_context(tc.psum_pool(name="psum_acc", bufs=1))

        ident_bf = const.tile([P, P], BF16)
        masks.make_identity(nc, ident_bf[:])
        ident_f32 = const.tile([P, P], F32)
        masks.make_identity(nc, ident_f32[:])
        log_bias = const.tile([P, 1], F32)
        nc.vector.memset(log_bias[:], NO_EDGE_LOG)
        big = const.tile([P, P], BF16)
        nc.vector.tensor_scalar_mul(out=big[:], in0=ident_bf[:], scalar1=2.0**100)
        ones = const.tile([P, 1], BF16)
        nc.vector.memset(ones[:], 1.0)

        foT = const.tile([P, H, N], BF16)
        fo_raw_of = {}

        def load_fo(hd, parts):
            fo_raw = raw.tile([P, TILES, D], BF16, tag="fo_raw")
            rows = f_other[hd, :, :].rearrange("(t p) d -> p t d", p=P)
            for part in range(parts):
                tiles = slice(part * TILES // parts, (part + 1) * TILES // parts)
                nc.sync.dma_start(out=fo_raw[:, tiles, :], in_=rows[:, tiles, :])
            fo_raw_of[hd] = fo_raw

        def turn_fo(hd, blk, psum, tag, copy):
            pt = psum.tile([P, 4, P], BF16, tag=tag)
            for k in range(4):
                nc.tensor.transpose(pt[:, k, :], fo_raw_of[hd][:, 4 * blk + k, :], ident_bf[:])
            copy(out=foT[:, hd, blk * BANK : (blk + 1) * BANK], in_=pt[:].rearrange("p k n -> p (k n)"))

        fs_raw_of = {}
        fs_turned_of = {}
        fsT_of = {}

        def load_fs(pair):
            fs_raw = fsp.tile([P, H, 2, D], BF16, tag="fs_raw")
            nodes = slice(2 * pair * P, 2 * (pair + 1) * P)
            nc.sync.dma_start(out=fs_raw[:], in_=f_self[:, nodes, :].rearrange("h (p e) d -> p h e d", e=2))
            fs_raw_of[pair] = fs_raw

        def turn_fs(tile_no):
            pt = psum_mask.tile([P, H, P], BF16, tag="zt")
            for hd in range(H):
                nc.tensor.transpose(pt[:, hd, :], fs_raw_of[tile_no // 2][:, hd, tile_no % 2, :], ident_bf[:])
            fs_turned_of[tile_no] = pt

        def negate_fs(tile_no):
            fsT = fsp.tile([P, H, P], BF16, tag="fsT")
            nc.vector.tensor_scalar_mul(out=fsT[:], in0=fs_turned_of[tile_no][:], scalar1=-1.0)
            fsT_of[tile_no] = fsT

        k_raw = setup.tile([P, H, PACK, O], BF16)
        k_grp = setup.tile([P, H, O, PACK], BF16, align_bytes=64)
        k_codes = setup.tile([P, H * O], U32, align_bytes=64)
        k_scales = setup.tile([P, H * O], U8, align_bytes=64)

        def load_kernel():
            for hd in range(H):
                nc.sync.dma_start(
                    out=k_raw[:, hd, :, :].rearrange("p (u e) o -> p u e o", u=2),
                    in_=kernel[hd, :, :].rearrange("(u p e) o -> p u e o", u=2, e=2),
                )

        def group_kernel():
            nc.vector.tensor_copy(out=k_grp[:], in_=k_raw[:].rearrange("p h t o -> p h o t"))

        def quantise_kernel():
            nc.vector.quantize_mx(
                out=k_codes[:].bitcast(FP8X4), scales=k_scales[:], in_=k_grp[:].rearrange("p h o t -> p (h o t)")
            )

        x_raw = setup.tile([P, TILES // 2, 2, F], BF16, tag="x_raw", align_bytes=64)
        x_grp = setup.tile([P, TILES * P * PACK], BF16, align_bytes=64)
        x_grp32 = x_grp[:].bitcast(F32).rearrange("p (t n u) -> p t n u", t=TILES, u=2)
        x_codes = setup.tile([P, TILES * P], U32, align_bytes=64)
        x_scales = setup.tile([P, TILES * P], U8, align_bytes=64)
        xt_of = {}
        zero_of = {}
        count_of = []
        rowmask = const.tile([P, TILES], F32)

        def load_x(part):
            pairs = slice(2 * part, 2 * part + 2)
            nc.sync.dma_start(out=x_raw[:, pairs, :, :], in_=x_rows[:, pairs, :, :])

        def turn_x(pair):
            xt = psum_tr.tile([P, 2, 2, P], F32, tag="tr")
            for e in range(2):
                words = x_raw[:, pair, e, :].bitcast(F32)
                for u in range(2):
                    nc.tensor.transpose(xt[:, e, u, :], words[:, u * P : (u + 1) * P], ident_f32[:])
            xt_of[pair] = xt

        def group_x(pair):
            nc.scalar.copy(
                out=x_grp32[:, 2 * pair : 2 * pair + 2, :, :], in_=xt_of[pair][:].rearrange("p t u n -> p t n u")
            )

        def quantise_x(half):
            words = slice(half * 1024, (half + 1) * 1024)
            nc.vector.quantize_mx(
                out=x_codes[:, words].bitcast(FP8X4),
                scales=x_scales[:, words],
                in_=x_grp[:, half * 4096 : (half + 1) * 4096],
            )

        def find_zeros(g):
            zero = zerop.tile([P, PACK, P, PACK], BF16, tag="zero")
            nc.vector.tensor_single_scalar(
                out=zero[:].rearrange("p t n k -> p (t n k)"),
                in_=x_grp[:, g * N : (g + 1) * N],
                scalar=0.0,
                op=ALU.is_equal,
            )
            zero_of[g] = zero

        def count_zeros(g):
            if g == 0:
                count = psum_acc.tile([P, TILES], F32, tag="acc")
                count_of.append(count)
            for t in range(PACK):
                tile_no = PACK * g + t
                for k in range(PACK):
                    nc.tensor.matmul(
                        count_of[0][:, tile_no : tile_no + 1],
                        lhsT=zero_of[g][:, t, :, k],
                        rhs=ones[:],
                        start=(k == 0),
                        stop=(k == PACK - 1),
                    )

        def mark_padding():
            nc.vector.tensor_single_scalar(out=rowmask[:], in_=count_of[0][:], scalar=float(F), op=ALU.is_lt)

        f_grp_of = []
        fb_of = {}
        f_codes = const.tile([P, PASSES, H, O], U32, align_bytes=64)
        f_scales = const.tile([P, PASSES, H, O], U8, align_bytes=64)

        def make_feats(g, hd):
            if g == 0 and hd == 0:
                f_grp = setup.tile([P, PASSES, H, O, PACK], BF16, tag="x_raw", align_bytes=64)
                f_grp_of.append(f_grp)
            fb = psum_tr.tile([P, PACK, O], F32, tag="tr")
            for t in range(PACK):
                nodes = slice((PACK * g + t) * P, (PACK * g + t + 1) * P)
                nc.tensor.matmul_mx(
                    out=fb[:, t, :],
                    lhsT=x_codes[:, nodes].bitcast(FP8X4),
                    lhsT_scale=x_scales[:, nodes],
                    rhs=k_codes[:, hd * O : (hd + 1) * O].bitcast(FP8X4),
                    rhs_scale=k_scales[:, hd * O : (hd + 1) * O],
                    start=True,
                    stop=True,
                )
            fb_of[g, hd] = fb

        def group_feats(g, hd):
            nc.scalar.copy(out=f_grp_of[0][:, g, hd, :, :], in_=fb_of[g, hd][:].rearrange("p t o -> p o t"))

        def quantise_feats(g):
            nc.vector.quantize_mx(
                out=f_codes[:, g, :, :].rearrange("p h o -> p (h o)").bitcast(FP8X4),
                scales=f_scales[:, g, :, :].rearrange("p h o -> p (h o)"),
                in_=f_grp_of[0][:, g, :, :, :].rearrange("p h o t -> p (h o t)"),
            )

        adj_of = {}
        is_zero_of = {}
        zt_of = {}
        mask_of = {}
        banks_of = {}
        t_of = {}
        z_of = {}
        top_of = {}
        bent_of = {}
        shift_of = {}
        em_of = {}
        tr_of = {}
        grp_of = {}
        codes_of = {}
        den_of = {}
        gain_of = {}
        acc_of = {}

        def load_adj(tile_no, parts):
            adj_t = adjp.tile([P, N], BF16, tag="adj")
            for part in range(parts):
                cols = slice(part * N // parts, (part + 1) * N // parts)
                nc.sync.dma_start(out=adj_t[:, cols], in_=adj_rows[tile_no // 2, tile_no % 2][:, cols])
            adj_of[tile_no] = adj_t

        def find_no_edge(tile_no, first, last):
            if first == 0:
                is_zero = edgep.tile([P, N], BF16, tag="is_zero")
                is_zero_of[tile_no] = is_zero
            cols = slice(first * BANK, last * BANK)
            nc.vector.tensor_single_scalar(
                out=is_zero_of[tile_no][:, cols], in_=adj_of[tile_no][:, cols], scalar=0.0, op=ALU.is_equal
            )

        def turn_adj(psum, tag, tile_no, blk):
            adj_t = adj_of[tile_no]
            zt = psum.tile([P, 4, P], BF16, tag=tag)
            for k in range(4):
                nc.tensor.transpose(zt[:, k, :], adj_t[:, (4 * blk + k) * P : (4 * blk + k + 1) * P], ident_bf[:])
            zt_of[tile_no, blk] = zt

        def make_mask(tile_no, blk):
            if tile_no not in mask_of:
                maskT = maskp.tile([P, TILES, P], F32, tag="maskT")
                mask_of[tile_no] = maskT
            nc.scalar.activation(
                out=mask_of[tile_no][:, 4 * blk : 4 * blk + 4, :],
                in_=zt_of[tile_no, blk][:],
                func=ACT.Exp,
                bias=log_bias[:, 0:1],
                scale=-EDGE_SLOPE,
            )

        def dense(i, banks):
            tile_no, hd = divmod(i, H)
            for q in banks:
                bank = psum_dense.tile([P, BANK], F32, tag="dense")
                nc.tensor.matmul(
                    bank[:],
                    lhsT=fsT_of[tile_no][:, hd, :],
                    rhs=foT[:, hd, q * BANK : (q + 1) * BANK],
                    start=True,
                    stop=False,
                )
                banks_of[i, q] = bank
            for q in banks:
                if CHUNKS * tile_no + q < PLAIN_BANKS:
                    cols = slice(q * BANK, (q + 1) * BANK)
                    nc.tensor.matmul(
                        banks_of[i, q][:], lhsT=big[:], rhs=is_zero_of[tile_no][:, cols], start=False, stop=True
                    )
                    continue
                for k in range(4):
                    nc.tensor.matmul(
                        banks_of[i, q][:, k * P : (k + 1) * P],
                        lhsT=mask_of[tile_no][:, 4 * q + k, :],
                        rhs=ident_f32[:],
                        is_transpose=True,
                        start=False,
                        stop=(k == 3),
                    )

        def weigh(i, q):
            if q == 0:
                t = tp.tile([P, N], F32, tag="t")
                t_of[i] = t
            cols = slice(q * BANK, (q + 1) * BANK)
            nc.vector.scalar_tensor_tensor(
                out=t_of[i][:, cols],
                in0=adj_of[i // H][:, cols],
                scalar=LEAST_WEIGHT,
                in1=banks_of[i, q][:],
                op0=ALU.max,
                op1=ALU.mult,
            )

        def own_cols(i):
            return LAST_OWN if i == UNITS - 1 else OWN

        def bend(i, first, last):
            t = t_of[i]
            if first == own_cols(i):
                z = zp.tile([P, N], F32, tag="z")
                z_of[i] = z
            cols = slice(first, last)
            nc.scalar.activation(out=z_of[i][:, cols], in_=t[:, cols], func=ACT.Relu, scale=1.0 - SLOPE)
            if last == N:
                cols = slice(own_cols(i), N)
                nc.gpsimd.tensor_tensor(out=z_of[i][:, cols], in0=t[:, cols], in1=z_of[i][:, cols], op=ALU.subtract)

        def bend_own(i):
            t = t_of[i]
            own = slice(0, own_cols(i))
            nc.vector.scalar_tensor_tensor(
                out=z_of[i][:, own], in0=t[:, own], scalar=SLOPE, in1=t[:, own], op0=ALU.mult, op1=ALU.min
            )

        def row_min(i):
            top = small.tile([P, 1], F32, tag="top")
            nc.vector.tensor_reduce(out=top[:], in_=t_of[i][:], axis=AX.X, op=ALU.min)
            top_of[i] = top

        def bend_min(i):
            top = top_of[i]
            bent = small.tile([P, 1], F32, tag="bent")
            nc.vector.tensor_scalar(
                out=bent[:], in0=top[:], scalar1=SLOPE, scalar2=top[:, 0:1], op0=ALU.mult, op1=ALU.min
            )
            bent_of[i] = bent

        def shift_min(i):
            shift = small.tile([P, 1], F32, tag="shift")
            nc.vector.tensor_scalar(
                out=shift[:], in0=bent_of[i][:], scalar1=CEILING, scalar2=SCALE, op0=ALU.min, op1=ALU.mult
            )
            shift_of[i] = shift

        def exponential(i):
            tile_no, hd = divmod(i, H)
            if hd == 0:
                den = small.tile([P, H], F32, tag="den")
                den_of[tile_no] = den
            em = emp.tile([P, N], BF16, tag="em")
            nc.scalar.activation(
                out=em[:],
                in_=z_of[i][:],
                func=ACT.Exp,
                bias=shift_of[i][:, 0:1],
                scale=-SCALE,
                accum_out=den_of[tile_no][:, hd : hd + 1],
            )
            em_of[i] = em

        def turn(i):
            words = em_of[i][:].bitcast(F32)
            for half in range(2):
                tr = psum_tr.tile([P, 2, 2, P], F32, tag="tr")
                for gg in range(2):
                    for u in range(2):
                        first = (2 * (2 * half + gg) + u) * P
                        nc.tensor.transpose(tr[:, gg, u, :], words[:, first : first + P], ident_f32[:])
                tr_of[i, half] = tr

        def group(i, half, drain):
            if half == 0:
                grp = emp.tile([P, N], BF16, tag="grp", align_bytes=64)
                grp_of[i] = grp
            grp32 = grp_of[i][:].bitcast(F32).rearrange("p (g n u) -> p g n u", g=PASSES, u=2)
            dst = grp32[:, 2 * half : 2 * half + 2, :, :]
            src = tr_of[i, half][:].rearrange("p g u n -> p g n u")
            if half == 1 and drain:
                nc.vector.tensor_copy(out=dst, in_=src)
            else:
                nc.scalar.copy(out=dst, in_=src)

        def quantise(i):
            codes = codep.tile([P, PASSES * P], U32, tag="codes", align_bytes=64)
            scales = codep.tile([P, PASSES * P], U8, tag="scales", align_bytes=64)
            nc.vector.quantize_mx(out=codes[:].bitcast(FP8X4), scales=scales[:], in_=grp_of[i][:])
            codes_of[i] = (codes, scales)

        def aggregate(i):
            tile_no, hd = divmod(i, H)
            codes, scales = codes_of[i]
            if hd == 0:
                acc = psum_acc.tile([P, H, O], F32, tag="acc")
                acc_of[tile_no] = acc
            for g in range(PASSES):
                nc.tensor.matmul_mx(
                    out=acc_of[tile_no][:, hd, :],
                    lhsT=codes[:, g * P : (g + 1) * P].bitcast(FP8X4),
                    lhsT_scale=scales[:, g * P : (g + 1) * P],
                    rhs=f_codes[:, g, hd, :].bitcast(FP8X4),
                    rhs_scale=f_scales[:, g, hd, :],
                    start=(g == 0),
                    stop=(g == PASSES - 1),
                )

        def gain_step(tile_no, part):
            if part == 0:
                gain = small.tile([P, H], F32, tag="gain")
                gain_of[tile_no] = gain
                nc.vector.tensor_scalar_max(out=gain[:], in0=den_of[tile_no][:], scalar1=TINY)
            elif part == 1:
                nc.vector.reciprocal(out=gain_of[tile_no][:], in_=gain_of[tile_no][:])
            else:
                nc.vector.tensor_scalar_mul(
                    out=gain_of[tile_no][:], in0=gain_of[tile_no][:], scalar1=rowmask[:, tile_no : tile_no + 1]
                )

        def finish(tile_no):
            o_sb = outp.tile([P, H, O], F32, tag="o_sb")
            for k in range(H):
                nc.scalar.activation(
                    out=o_sb[:, k, :],
                    in_=acc_of[tile_no][:, k, :],
                    func=ACT.Relu,
                    scale=gain_of[tile_no][:, k : k + 1],
                )
            nc.sync.dma_start(out=out_rows[tile_no // 2, tile_no % 2], in_=o_sb[:].rearrange("p h o -> p (h o)"))

        load_fo(0, 2)
        load_fs(0)
        load_adj(0, 2)
        load_fo(1, 1)
        load_adj(1, 1)
        load_fo(2, 1)
        load_fo(3, 1)
        load_kernel()
        for part in range(TILES // 4):
            load_x(part)
        engines = {mybir.EngineType.PE, mybir.EngineType.DVE, mybir.EngineType.Activation, mybir.EngineType.Pool}
        with tc.manual_schedule(engines=engines):
            for blk in range(TILES // 4):
                if blk == 2:
                    turn_fo(0, blk, psum_acc, "acc", nc.vector.tensor_copy)
                else:
                    turn_fo(0, blk, psum_tr, "tr", nc.vector.tensor_copy)
            turn_fs(0)
            negate_fs(0)
            find_no_edge(0, 0, 2)
            find_no_edge(0, 2, 4)
            for q in range(CHUNKS):
                dense(0, (q,))
                if q % 2 == 1:
                    turn_fo(1, q - 1, psum_tr, "tr", nc.scalar.copy)
                    turn_fo(1, q, psum_tr, "tr", nc.scalar.copy)
            waiting = []
            finished = 0
            for step in range(UNITS + 4):
                tile_no, hd = divmod(step, H)
                live = step < UNITS
                ahead = step + H + 1
                gain_now = tile_no > 0 and hd == (3 if live else 2)
                if hd == 0 and tile_no + 2 < TILES:
                    load_adj(tile_no + 2, 1)
                    if tile_no % 2 == 0:
                        load_fs(tile_no // 2 + 1)
                if live:
                    weigh(step, 0)
                if hd == 3 and tile_no + 1 < TILES:
                    negate_fs(tile_no + 1)
                if PLAIN_BANKS <= ahead < UNITS:
                    turn_adj(psum_mask, "zt", ahead // H, ahead % H)
                if 0 <= step - 3 < UNITS and live:
                    group(step - 3, 0, not live)
                    group(step - 3, 1, not live)
                if live:
                    weigh(step, 1)
                if step + 1 < UNITS:
                    dense(step + 1, (0, 1))
                if step == 7:
                    mark_padding()
                if 0 <= step - 1 < UNITS:
                    bend_min(step - 1)
                if gain_now:
                    gain_step(tile_no - 1, 0)
                if 2 <= step < 2 + TILES // 4:
                    turn_x(2 * step - 4)
                    turn_x(2 * step - 3)
                feats = divmod(step - FEATS_START, 2)
                if 0 <= feats[0] < PASSES:
                    make_feats(feats[0], 2 * feats[1])
                    make_feats(feats[0], 2 * feats[1] + 1)
                if live:
                    weigh(step, 2)
                    bend(step, own_cols(step), 3 * BANK)
                if 0 <= step - 1 < UNITS:
                    shift_min(step - 1)
                if gain_now:
                    gain_step(tile_no - 1, 1)
                if live:
                    weigh(step, 3)
                if 0 <= step - 4 < UNITS and not live:
                    quantise(step - 4)
                    waiting.append(step - 4)
                if 0 <= step - 3 < UNITS and not live:
                    group(step - 3, 0, not live)
                    group(step - 3, 1, not live)
                if step + 1 < UNITS:
                    dense(step + 1, (2, 3))
                if 2 <= step < 2 + TILES // 4:
                    group_x(2 * step - 4)
                    group_x(2 * step - 3)
                if 0 <= feats[0] < PASSES:
                    group_feats(feats[0], 2 * feats[1])
                    group_feats(feats[0], 2 * feats[1] + 1)
                if live:
                    bend(step, 3 * BANK, N)
                if PLAIN_BANKS <= ahead < UNITS:
                    make_mask(ahead // H, ahead % H)
                if step < 2:
                    for blk in range(TILES // 4):
                        turn_fo(step + 2, blk, psum_tr, "tr", nc.scalar.copy)
                if gain_now:
                    gain_step(tile_no - 1, 2)
                if 0 <= step - 4 < UNITS and live:
                    quantise(step - 4)
                    waiting.append(step - 4)
                if live:
                    bend_own(step)
                if step == 0:
                    find_no_edge(1, 0, PLAIN_BANKS - CHUNKS)
                if step == 1:
                    group_kernel()
                if step == 2:
                    quantise_kernel()
                if step in (4, 7):
                    quantise_x((step - 4) // 3)
                if 3 <= step < 3 + PASSES:
                    find_zeros(step - 3)
                if 0 < step - FEATS_START <= 2 * PASSES and (step - FEATS_START) % 2 == 0:
                    quantise_feats((step - FEATS_START) // 2 - 1)
                if live:
                    row_min(step)
                if 3 <= step < 3 + PASSES:
                    count_zeros(step - 3)
                ready = step > FEATS_START + 2 * PASSES
                units = [unit for unit in waiting[:2] if ready and unit // H == finished]
                waiting = waiting[len(units) :]
                for unit in units:
                    aggregate(unit)
                if 0 <= step - 2 < UNITS:
                    turn(step - 2)
                if hd == 2 and tile_no + 1 < TILES:
                    turn_fs(tile_no + 1)
                if 0 <= step - 1 < UNITS:
                    exponential(step - 1)
                if units and units[-1] % H == H - 1:
                    finish(finished)
                    finished += 1
